import numpy as np
import ml_dtypes


def mxq(x, axis, fmt="e4m3"):
    dtype, down = {"e4m3": (ml_dtypes.float8_e4m3fn, 7), "e5m2": (ml_dtypes.float8_e5m2, 14)}[fmt]
    v = np.moveaxis(np.asarray(x, np.float32).astype(ml_dtypes.bfloat16).astype(np.float64), axis, -1)
    blocks = v.reshape(v.shape[:-1] + (-1, 32))
    amax = np.abs(blocks).max(-1, keepdims=True)
    byte = np.maximum(np.where(amax > 0, np.frexp(amax)[1] - 1 + 127, 0) - down, 1)
    scale = np.exp2(byte - 127.0)
    codes = (blocks / scale).astype(np.float32).astype(dtype).astype(np.float64)
    return np.moveaxis((codes * scale).reshape(v.shape), -1, axis)


WIDE = False


def mx_kscale(k):
    if not WIDE:
        return np.ones(k)
    levels = np.array([10, -10, 5, -5, 0])
    a = np.random.permutation(np.resize(levels, k // 512 * 4)).reshape(k // 512, 4)
    idx = np.arange(k)
    return np.exp2(a[idx // 512, idx % 128 // 32])


BF16 = ml_dtypes.bfloat16


def bf(x):
    return np.asarray(x, np.float32).astype(BF16)


def f64(x):
    return np.asarray(x).astype(np.float64)


B, T, C, HS = 16, 512, 1024, 128
D2 = HS // 2


def rope_tables():
    i = np.arange(D2, dtype=np.float64)
    theta = 10000.0 ** (-2.0 * (i - 1.0) / D2)
    ang = np.arange(T, dtype=np.float64)[:, None] * theta[None, :]
    return np.cos(ang), np.sin(ang)


def rotate(t, c, s):
    e, o = t[..., 0::2], t[..., 1::2]
    return np.stack([e * c + o * s, -e * s + o * c], axis=-1).reshape(t.shape)


def setup_inputs():
    s = mx_kscale(C)
    return {"x": bf(np.random.standard_normal((B, T, C)) * s),
            "Wq": bf(np.random.standard_normal((C, HS)) / np.sqrt(C) / s[:, None]),
            "Wk": bf(np.random.standard_normal((C, HS)) / np.sqrt(C) / s[:, None])}


def reference(x, Wq, Wk):
    c, s = rope_tables()
    xq = mxq(f64(x), 2, "e4m3")
    q_rot = rotate(xq @ mxq(f64(Wq), 0, "e4m3"), c, s)
    k_rot = rotate(xq @ mxq(f64(Wk), 0, "e4m3"), c, s)
    return q_rot, k_rot

@@ -1,0 +1,229 @@
+from contextlib import ExitStack
+import math
+
+import concourse.mybir as mybir
+from concourse.masks import make_identity
+
+F32 = mybir.dt.float32
+BF16 = mybir.dt.bfloat16
+U32 = mybir.dt.uint32
+U8 = mybir.dt.uint8
+FP8X4 = mybir.dt.float8_e4m3fn_x4
+ALU = mybir.AluOpType
+ACT = mybir.ActivationFunctionType
+
+BATCH, TOKENS, CHANNELS, HEAD = 16, 512, 1024, 128
+P = 128
+PACK = 4
+PASSES = CHANNELS // (P * PACK)
+ROWS = TOKENS // P
+PAIRS = HEAD // 2
+FEATURES = 2 * HEAD
+WORDS = CHANNELS // 2
+TILE_COLS = PASSES * P
+TILES_PER_BANK = 2
+BANKS = ROWS // TILES_PER_BANK
+X_CHUNKS_IN_SBUF = 8
+
+FLOPS = 2 * BATCH * TOKENS * CHANNELS * FEATURES
+
+RATIO = 10000.0 ** (-2.0 / PAIRS)
+ROUND_TO_WHOLE = 1.5 * 2**23
+
+
+def half_angle_squares(nc, pool):
+    position = pool.tile([P, ROWS], F32)
+    nc.gpsimd.iota(
+        position[:],
+        pattern=[[1, ROWS]],
+        base=0,
+        channel_multiplier=ROWS,
+        allow_small_or_imprecise_dtypes=True,
+    )
+    powers = pool.tile([P, PAIRS], F32)
+    nc.vector.memset(powers[:, 0:1], 1.0)
+    filled = 1
+    while filled < PAIRS:
+        nc.vector.tensor_scalar_mul(
+            out=powers[:, filled : 2 * filled], in0=powers[:, 0:filled], scalar1=RATIO**filled
+        )
+        filled *= 2
+    shape = [P, ROWS, PAIRS]
+    turns = pool.tile(shape, F32)
+    nc.vector.scalar_tensor_tensor(
+        out=turns[:],
+        in0=powers[:].unsqueeze(1).to_broadcast(shape),
+        scalar=1.0 / (RATIO * 2.0 * math.pi),
+        in1=position[:].unsqueeze(2).to_broadcast(shape),
+        op0=ALU.mult,
+        op1=ALU.mult,
+    )
+    whole = pool.tile(shape, F32)
+    nc.vector.tensor_scalar_add(out=whole[:], in0=turns[:], scalar1=ROUND_TO_WHOLE)
+    half = pool.tile([P, 2, ROWS, PAIRS], F32)
+    nc.vector.scalar_tensor_tensor(
+        out=half[:, 0], in0=whole[:], scalar=ROUND_TO_WHOLE, in1=turns[:], op0=ALU.subtract, op1=ALU.subtract
+    )
+    nc.vector.tensor_scalar_add(out=half[:, 1], in0=half[:, 0], scalar1=0.25)
+    nc.scalar.activation(out=half[:], in_=half[:], func=ACT.Sin, scale=math.pi)
+    nc.scalar.activation(out=half[:], in_=half[:], func=ACT.Square)
+    return half
+
+
+def fill_rotation_table(nc, half, table):
+    for row, column in ((0, 0), (1, 1)):
+        nc.vector.tensor_scalar(
+            out=table[:, :, row, column, :], in0=half[:, 0], scalar1=-2.0, scalar2=1.0, op0=ALU.mult, op1=ALU.add
+        )
+    nc.vector.tensor_scalar(
+        out=table[:, :, 0, 1, :], in0=half[:, 1], scalar1=-2.0, scalar2=1.0, op0=ALU.mult, op1=ALU.add
+    )
+    nc.vector.tensor_scalar(
+        out=table[:, :, 1, 0, :], in0=half[:, 1], scalar1=2.0, scalar2=-1.0, op0=ALU.mult, op1=ALU.add
+    )
+
+
+def load_weights(nc, pool, weights):
+    w_rows = pool.tile([P, 2, PASSES * PACK, HEAD], BF16)
+    for w, weight in enumerate(weights):
+        nc.scalar.dma_start(
+            out=w_rows[:, w].rearrange("p (c e) f -> p c (e f)", e=2),
+            in_=weight.rearrange("(c p e) f -> p c (e f)", p=P, e=2),
+        )
+    return w_rows
+
+
+def quantise_weights(nc, pool, w_rows, w_codes, w_scales):
+    w_grouped = pool.tile([P, PASSES, 2, 2, PAIRS, PACK], BF16, align_bytes=64)
+    for g in range(PASSES):
+        for w in range(2):
+            nc.vector.tensor_copy(
+                out=w_grouped[:, g, w],
+                in_=w_rows[:, w, PACK * g : PACK * (g + 1), :].rearrange("p t (i h) -> p h i t", h=2),
+            )
+    nc.vector.quantize_mx(
+        out=w_codes[:].bitcast(FP8X4),
+        scales=w_scales[:],
+        in_=w_grouped[:].rearrange("p g w h i t -> p (g w h i t)"),
+    )
+
+
+def tile_head_pa_kernel(tc, x, Wq, Wk, out_0, out_1):
+    nc = tc.nc
+    with ExitStack() as ctx:
+        ctx.enter_context(tc.manual_schedule())
+        const = ctx.enter_context(tc.tile_pool(name="const", bufs=1))
+        x_pool = ctx.enter_context(tc.tile_pool(name="x", bufs=X_CHUNKS_IN_SBUF))
+        grouped_pool = ctx.enter_context(tc.tile_pool(name="grouped", bufs=3))
+        codes_pool = ctx.enter_context(tc.tile_pool(name="codes", bufs=3))
+        products_pool = ctx.enter_context(tc.tile_pool(name="products", bufs=3))
+        rotated_pool = ctx.enter_context(tc.tile_pool(name="rotated", bufs=4))
+        transposed_pool = ctx.enter_context(tc.psum_pool(name="transposed", bufs=ROWS))
+        sums_pool = ctx.enter_context(tc.psum_pool(name="sums", bufs=2 * BANKS))
+
+        x_tiles = {}
+        grouped_tiles = {}
+        codes_tiles = {}
+        sums_tiles = {}
+
+        def load(b):
+            x_rows = x_pool.tile([P, ROWS * CHANNELS], BF16)
+            pieces = ROWS if b == 0 else 1
+            width = ROWS * CHANNELS // pieces
+            for piece in range(pieces):
+                columns = slice(width * piece, width * (piece + 1))
+                nc.sync.dma_start(
+                    out=x_rows[:, columns], in_=x[b].rearrange("(p r) k -> p (r k)", r=ROWS)[:, columns]
+                )
+            x_tiles[b] = x_rows
+
+        def transpose(b):
+            x_words = x_tiles[b][:].bitcast(F32)
+            grouped = grouped_pool.tile([P, ROWS * TILE_COLS * PACK], BF16, align_bytes=64)
+            grouped_words = grouped[:].bitcast(F32)
+            for r in range(ROWS):
+                transposed = transposed_pool.tile([P, WORDS // P, P], F32)
+                for j in range(WORDS // P):
+                    first = WORDS * r + P * j
+                    nc.tensor.transpose(transposed[:, j, :], x_words[:, first : first + P], identity[:])
+                nc.scalar.copy(
+                    out=grouped_words[:, 2 * TILE_COLS * r : 2 * TILE_COLS * (r + 1)].rearrange(
+                        "p (g c u) -> p g c u", g=PASSES, u=2
+                    ),
+                    in_=transposed[:].rearrange("p (g u) c -> p g c u", u=2),
+                )
+            grouped_tiles[b] = grouped
+
+        def quantise(b):
+            codes = codes_pool.tile([P, ROWS * TILE_COLS], U32, align_bytes=64)
+            scales = codes_pool.tile([P, ROWS * TILE_COLS], U8, align_bytes=64)
+            nc.vector.quantize_mx(out=codes[:].bitcast(FP8X4), scales=scales[:], in_=grouped_tiles[b][:])
+            codes_tiles[b] = (codes, scales)
+
+        def project(b):
+            codes, scales = codes_tiles[b]
+            sums_tiles[b] = []
+            for o in range(BANKS):
+                sums = sums_pool.tile([P, TILES_PER_BANK, FEATURES], F32)
+                for n in range(TILES_PER_BANK):
+                    for g in range(PASSES):
+                        first = TILE_COLS * (TILES_PER_BANK * o + n) + P * g
+                        nc.tensor.matmul_mx(
+                            out=sums[:, n, :],
+                            lhsT=codes[:, first : first + P].bitcast(FP8X4),
+                            lhsT_scale=scales[:, first : first + P],
+                            rhs=w_codes[:, FEATURES * g : FEATURES * (g + 1)].bitcast(FP8X4),
+                            rhs_scale=w_scales[:, FEATURES * g : FEATURES * (g + 1)],
+                            start=(g == 0),
+                            stop=(g == PASSES - 1),
+                        )
+                sums_tiles[b].append(sums)
+
+        def rotate(b):
+            products = products_pool.tile([P, ROWS, 2, 2, HEAD], F32)
+            for o in range(BANKS):
+                rows = slice(TILES_PER_BANK * o, TILES_PER_BANK * (o + 1))
+                shape = [P, TILES_PER_BANK, 2, 2, HEAD]
+                nc.vector.tensor_tensor(
+                    out=products[:, rows],
+                    in0=sums_tiles[b][o][:].rearrange("p n (w f) -> p n w f", w=2).unsqueeze(3).to_broadcast(shape),
+                    in1=table[:, rows].rearrange("p n a h i -> p n a (h i)").unsqueeze(2).to_broadcast(shape),
+                    op=ALU.mult,
+                )
+            rotated = rotated_pool.tile([P, 2, ROWS, HEAD], F32)
+            nc.gpsimd.tensor_tensor(
+                out=rotated[:].rearrange("p w r (i h) -> p r w i h", h=2),
+                in0=products[:, :, :, :, 0:PAIRS].rearrange("p r w h i -> p r w i h"),
+                in1=products[:, :, :, :, PAIRS:HEAD].rearrange("p r w h i -> p r w i h"),
+                op=ALU.add,
+            )
+            for w, out in enumerate((out_0, out_1)):
+                nc.sync.dma_start(
+                    out=out[b].rearrange("(p r) f -> p (r f)", r=ROWS),
+                    in_=rotated[:, w].rearrange("p r f -> p (r f)"),
+                )
+
+        w_codes = const.tile([P, PASSES * FEATURES], U32, align_bytes=64)
+        w_scales = const.tile([P, PASSES * FEATURES], U8, align_bytes=64)
+        table = const.tile([P, ROWS, 2, 2, PAIRS], F32)
+        identity = const.tile([P, P], F32)
+
+        w_rows = load_weights(nc, const, (Wq, Wk))
+        for b in range(X_CHUNKS_IN_SBUF):
+            load(b)
+        half = half_angle_squares(nc, const)
+        make_identity(nc, identity[:])
+        quantise_weights(nc, const, w_rows, w_codes, w_scales)
+        fill_rotation_table(nc, half, table)
+
+        transpose(0)
+        quantise(0)
+        for b in range(BATCH):
+            if b + 1 < BATCH:
+                transpose(b + 1)
+            project(b)
+            if b + 1 < BATCH:
+                quantise(b + 1)
+            rotate(b)
+            if b + X_CHUNKS_IN_SBUF < BATCH:
+                load(b + X_CHUNKS_IN_SBUF)

@@ -21,8 +21,9 @@ PAIRS = HEAD // 2
 FEATURES = 2 * HEAD
 WORDS = CHANNELS // 2
 TILE_COLS = PASSES * P
-TILES_PER_BANK = 2
-BANKS = ROWS // TILES_PER_BANK
+UNIT_TILES = 2
+CHUNK_UNITS = ROWS // UNIT_TILES
+UNITS = BATCH * CHUNK_UNITS
 X_CHUNKS_IN_SBUF = 8
 
 FLOPS = 2 * BATCH * TOKENS * CHANNELS * FEATURES
@@ -114,17 +115,18 @@ def tile_head_pa_kernel(tc, x, Wq, Wk, out_0, out_1):
         ctx.enter_context(tc.manual_schedule())
         const = ctx.enter_context(tc.tile_pool(name="const", bufs=1))
         x_pool = ctx.enter_context(tc.tile_pool(name="x", bufs=X_CHUNKS_IN_SBUF))
-        grouped_pool = ctx.enter_context(tc.tile_pool(name="grouped", bufs=3))
-        codes_pool = ctx.enter_context(tc.tile_pool(name="codes", bufs=3))
+        grouped_pool = ctx.enter_context(tc.tile_pool(name="grouped", bufs=4))
+        codes_pool = ctx.enter_context(tc.tile_pool(name="codes", bufs=4))
         products_pool = ctx.enter_context(tc.tile_pool(name="products", bufs=3))
         rotated_pool = ctx.enter_context(tc.tile_pool(name="rotated", bufs=4))
-        transposed_pool = ctx.enter_context(tc.psum_pool(name="transposed", bufs=ROWS))
-        sums_pool = ctx.enter_context(tc.psum_pool(name="sums", bufs=2 * BANKS))
+        transposed_pool = ctx.enter_context(tc.psum_pool(name="transposed", bufs=2 * UNIT_TILES))
+        sums_pool = ctx.enter_context(tc.psum_pool(name="sums", bufs=4))
 
         x_tiles = {}
         grouped_tiles = {}
         codes_tiles = {}
         sums_tiles = {}
+        products_tiles = {}
 
         def load(b):
             x_rows = x_pool.tile([P, ROWS * CHANNELS], BF16)
@@ -137,59 +139,64 @@ def tile_head_pa_kernel(tc, x, Wq, Wk, out_0, out_1):
                 )
             x_tiles[b] = x_rows
 
-        def transpose(b):
-            x_words = x_tiles[b][:].bitcast(F32)
-            grouped = grouped_pool.tile([P, ROWS * TILE_COLS * PACK], BF16, align_bytes=64)
+        def transpose(unit):
+            x_words = x_tiles[unit // CHUNK_UNITS][:].bitcast(F32)
+            grouped = grouped_pool.tile([P, UNIT_TILES * TILE_COLS * PACK], BF16, align_bytes=64)
             grouped_words = grouped[:].bitcast(F32)
-            for r in range(ROWS):
+            for n in range(UNIT_TILES):
+                r = UNIT_TILES * (unit % CHUNK_UNITS) + n
                 transposed = transposed_pool.tile([P, WORDS // P, P], F32)
                 for j in range(WORDS // P):
                     first = WORDS * r + P * j
                     nc.tensor.transpose(transposed[:, j, :], x_words[:, first : first + P], identity[:])
                 nc.scalar.copy(
-                    out=grouped_words[:, 2 * TILE_COLS * r : 2 * TILE_COLS * (r + 1)].rearrange(
+                    out=grouped_words[:, 2 * TILE_COLS * n : 2 * TILE_COLS * (n + 1)].rearrange(
                         "p (g c u) -> p g c u", g=PASSES, u=2
                     ),
                     in_=transposed[:].rearrange("p (g u) c -> p g c u", u=2),
                 )
-            grouped_tiles[b] = grouped
+            grouped_tiles[unit] = grouped
 
-        def quantise(b):
-            codes = codes_pool.tile([P, ROWS * TILE_COLS], U32, align_bytes=64)
-            scales = codes_pool.tile([P, ROWS * TILE_COLS], U8, align_bytes=64)
-            nc.vector.quantize_mx(out=codes[:].bitcast(FP8X4), scales=scales[:], in_=grouped_tiles[b][:])
-            codes_tiles[b] = (codes, scales)
+        def quantise(unit):
+            codes = codes_pool.tile([P, UNIT_TILES * TILE_COLS], U32, align_bytes=64)
+            scales = codes_pool.tile([P, UNIT_TILES * TILE_COLS], U8, align_bytes=64)
+            nc.vector.quantize_mx(out=codes[:].bitcast(FP8X4), scales=scales[:], in_=grouped_tiles[unit][:])
+            codes_tiles[unit] = (codes, scales)
 
-        def project(b):
-            codes, scales = codes_tiles[b]
-            sums_tiles[b] = []
-            for o in range(BANKS):
-                sums = sums_pool.tile([P, TILES_PER_BANK, FEATURES], F32)
-                for n in range(TILES_PER_BANK):
-                    for g in range(PASSES):
-                        first = TILE_COLS * (TILES_PER_BANK * o + n) + P * g
-                        nc.tensor.matmul_mx(
-                            out=sums[:, n, :],
-                            lhsT=codes[:, first : first + P].bitcast(FP8X4),
-                            lhsT_scale=scales[:, first : first + P],
-                            rhs=w_codes[:, FEATURES * g : FEATURES * (g + 1)].bitcast(FP8X4),
-                            rhs_scale=w_scales[:, FEATURES * g : FEATURES * (g + 1)],
-                            start=(g == 0),
-                            stop=(g == PASSES - 1),
-                        )
-                sums_tiles[b].append(sums)
+        def project(unit):
+            codes, scales = codes_tiles[unit]
+            sums = sums_pool.tile([P, UNIT_TILES, FEATURES], F32)
+            for n in range(UNIT_TILES):
+                for g in range(PASSES):
+                    first = TILE_COLS * n + P * g
+                    nc.tensor.matmul_mx(
+                        out=sums[:, n, :],
+                        lhsT=codes[:, first : first + P].bitcast(FP8X4),
+                        lhsT_scale=scales[:, first : first + P],
+                        rhs=w_codes[:, FEATURES * g : FEATURES * (g + 1)].bitcast(FP8X4),
+                        rhs_scale=w_scales[:, FEATURES * g : FEATURES * (g + 1)],
+                        start=(g == 0),
+                        stop=(g == PASSES - 1),
+                    )
+            sums_tiles[unit] = sums
 
-        def rotate(b):
-            products = products_pool.tile([P, ROWS, 2, 2, HEAD], F32)
-            for o in range(BANKS):
-                rows = slice(TILES_PER_BANK * o, TILES_PER_BANK * (o + 1))
-                shape = [P, TILES_PER_BANK, 2, 2, HEAD]
-                nc.vector.tensor_tensor(
-                    out=products[:, rows],
-                    in0=sums_tiles[b][o][:].rearrange("p n (w f) -> p n w f", w=2).unsqueeze(3).to_broadcast(shape),
-                    in1=table[:, rows].rearrange("p n a h i -> p n a (h i)").unsqueeze(2).to_broadcast(shape),
-                    op=ALU.mult,
-                )
+        def multiply(unit):
+            b = unit // CHUNK_UNITS
+            if unit % CHUNK_UNITS == 0:
+                products = products_pool.tile([P, ROWS, 2, 2, HEAD], F32)
+                products_tiles[b] = products
+            first = UNIT_TILES * (unit % CHUNK_UNITS)
+            rows = slice(first, first + UNIT_TILES)
+            shape = [P, UNIT_TILES, 2, 2, HEAD]
+            nc.vector.tensor_tensor(
+                out=products_tiles[b][:, rows],
+                in0=sums_tiles[unit][:].rearrange("p n (w f) -> p n w f", w=2).unsqueeze(3).to_broadcast(shape),
+                in1=table[:, rows].rearrange("p n a h i -> p n a (h i)").unsqueeze(2).to_broadcast(shape),
+                op=ALU.mult,
+            )
+
+        def add_and_store(b):
+            products = products_tiles[b]
             rotated = rotated_pool.tile([P, 2, ROWS, HEAD], F32)
             nc.gpsimd.tensor_tensor(
                 out=rotated[:].rearrange("p w r (i h) -> p r w i h", h=2),
@@ -217,13 +224,17 @@ def tile_head_pa_kernel(tc, x, Wq, Wk, out_0, out_1):
         fill_rotation_table(nc, half, table)
 
         transpose(0)
+        transpose(1)
         quantise(0)
-        for b in range(BATCH):
-            if b + 1 < BATCH:
-                transpose(b + 1)
-            project(b)
-            if b + 1 < BATCH:
-                quantise(b + 1)
-            rotate(b)
-            if b + X_CHUNKS_IN_SBUF < BATCH:
-                load(b + X_CHUNKS_IN_SBUF)
+        for unit in range(UNITS):
+            if unit + 2 < UNITS:
+                transpose(unit + 2)
+            project(unit)
+            if unit + 1 < UNITS:
+                quantise(unit + 1)
+            multiply(unit)
+            if unit % CHUNK_UNITS == CHUNK_UNITS - 1:
+                b = unit // CHUNK_UNITS
+                add_and_store(b)
+                if b + X_CHUNKS_IN_SBUF < BATCH:
+                    load(b + X_CHUNKS_IN_SBUF)

@@ -21,9 +21,8 @@ PAIRS = HEAD // 2
 FEATURES = 2 * HEAD
 WORDS = CHANNELS // 2
 TILE_COLS = PASSES * P
-UNIT_TILES = 2
-CHUNK_UNITS = ROWS // UNIT_TILES
-UNITS = BATCH * CHUNK_UNITS
+TILES_PER_BANK = 2
+BANKS = ROWS // TILES_PER_BANK
 X_CHUNKS_IN_SBUF = 8
 
 FLOPS = 2 * BATCH * TOKENS * CHANNELS * FEATURES
@@ -115,18 +114,17 @@ def tile_head_pa_kernel(tc, x, Wq, Wk, out_0, out_1):
         ctx.enter_context(tc.manual_schedule())
         const = ctx.enter_context(tc.tile_pool(name="const", bufs=1))
         x_pool = ctx.enter_context(tc.tile_pool(name="x", bufs=X_CHUNKS_IN_SBUF))
-        grouped_pool = ctx.enter_context(tc.tile_pool(name="grouped", bufs=4))
-        codes_pool = ctx.enter_context(tc.tile_pool(name="codes", bufs=4))
+        grouped_pool = ctx.enter_context(tc.tile_pool(name="grouped", bufs=3))
+        codes_pool = ctx.enter_context(tc.tile_pool(name="codes", bufs=3))
         products_pool = ctx.enter_context(tc.tile_pool(name="products", bufs=3))
         rotated_pool = ctx.enter_context(tc.tile_pool(name="rotated", bufs=4))
-        transposed_pool = ctx.enter_context(tc.psum_pool(name="transposed", bufs=2 * UNIT_TILES))
-        sums_pool = ctx.enter_context(tc.psum_pool(name="sums", bufs=4))
+        transposed_pool = ctx.enter_context(tc.psum_pool(name="transposed", bufs=ROWS))
+        sums_pool = ctx.enter_context(tc.psum_pool(name="sums", bufs=2 * BANKS))
 
         x_tiles = {}
         grouped_tiles = {}
         codes_tiles = {}
         sums_tiles = {}
-        products_tiles = {}
 
         def load(b):
             x_rows = x_pool.tile([P, ROWS * CHANNELS], BF16)
@@ -139,71 +137,68 @@ def tile_head_pa_kernel(tc, x, Wq, Wk, out_0, out_1):
                 )
             x_tiles[b] = x_rows
 
-        def transpose(unit):
-            x_words = x_tiles[unit // CHUNK_UNITS][:].bitcast(F32)
-            grouped = grouped_pool.tile([P, UNIT_TILES * TILE_COLS * PACK], BF16, align_bytes=64)
+        def transpose(b):
+            x_words = x_tiles[b][:].bitcast(F32)
+            grouped = grouped_pool.tile([P, ROWS * TILE_COLS * PACK], BF16, align_bytes=64)
             grouped_words = grouped[:].bitcast(F32)
-            for n in range(UNIT_TILES):
-                r = UNIT_TILES * (unit % CHUNK_UNITS) + n
+            for r in range(ROWS):
                 transposed = transposed_pool.tile([P, WORDS // P, P], F32)
                 for j in range(WORDS // P):
                     first = WORDS * r + P * j
                     nc.tensor.transpose(transposed[:, j, :], x_words[:, first : first + P], identity[:])
                 nc.scalar.copy(
-                    out=grouped_words[:, 2 * TILE_COLS * n : 2 * TILE_COLS * (n + 1)].rearrange(
+                    out=grouped_words[:, 2 * TILE_COLS * r : 2 * TILE_COLS * (r + 1)].rearrange(
                         "p (g c u) -> p g c u", g=PASSES, u=2
                     ),
                     in_=transposed[:].rearrange("p (g u) c -> p g c u", u=2),
                 )
-            grouped_tiles[unit] = grouped
+            grouped_tiles[b] = grouped
 
-        def quantise(unit):
-            codes = codes_pool.tile([P, UNIT_TILES * TILE_COLS], U32, align_bytes=64)
-            scales = codes_pool.tile([P, UNIT_TILES * TILE_COLS], U8, align_bytes=64)
-            nc.vector.quantize_mx(out=codes[:].bitcast(FP8X4), scales=scales[:], in_=grouped_tiles[unit][:])
-            codes_tiles[unit] = (codes, scales)
+        def quantise(b):
+            codes = codes_pool.tile([P, ROWS * TILE_COLS], U32, align_bytes=64)
+            scales = codes_pool.tile([P, ROWS * TILE_COLS], U8, align_bytes=64)
+            nc.vector.quantize_mx(out=codes[:].bitcast(FP8X4), scales=scales[:], in_=grouped_tiles[b][:])
+            codes_tiles[b] = (codes, scales)
 
-        def project(unit):
-            codes, scales = codes_tiles[unit]
-            sums = sums_pool.tile([P, UNIT_TILES, FEATURES], F32)
-            for n in range(UNIT_TILES):
-                for g in range(PASSES):
-                    first = TILE_COLS * n + P * g
-                    nc.tensor.matmul_mx(
-                        out=sums[:, n, :],
-                        lhsT=codes[:, first : first + P].bitcast(FP8X4),
-                        lhsT_scale=scales[:, first : first + P],
-                        rhs=w_codes[:, FEATURES * g : FEATURES * (g + 1)].bitcast(FP8X4),
-                        rhs_scale=w_scales[:, FEATURES * g : FEATURES * (g + 1)],
-                        start=(g == 0),
-                        stop=(g == PASSES - 1),
-                    )
-            sums_tiles[unit] = sums
+        def project(b):
+            codes, scales = codes_tiles[b]
+            sums_tiles[b] = []
+            for o in range(BANKS):
+                sums = sums_pool.tile([P, TILES_PER_BANK, FEATURES], F32)
+                for n in range(TILES_PER_BANK):
+                    for g in range(PASSES):
+                        first = TILE_COLS * (TILES_PER_BANK * o + n) + P * g
+                        nc.tensor.matmul_mx(
+                            out=sums[:, n, :],
+                            lhsT=codes[:, first : first + P].bitcast(FP8X4),
+                            lhsT_scale=scales[:, first : first + P],
+                            rhs=w_codes[:, FEATURES * g : FEATURES * (g + 1)].bitcast(FP8X4),
+                            rhs_scale=w_scales[:, FEATURES * g : FEATURES * (g + 1)],
+                            start=(g == 0),
+                            stop=(g == PASSES - 1),
+                        )
+                sums_tiles[b].append(sums)
 
-        def multiply(unit):
-            b = unit // CHUNK_UNITS
-            if unit % CHUNK_UNITS == 0:
-                products = products_pool.tile([P, ROWS, 2, 2, HEAD], F32)
-                products_tiles[b] = products
-            first = UNIT_TILES * (unit % CHUNK_UNITS)
-            rows = slice(first, first + UNIT_TILES)
-            shape = [P, UNIT_TILES, 2, 2, HEAD]
-            nc.vector.tensor_tensor(
-                out=products_tiles[b][:, rows],
-                in0=sums_tiles[unit][:].rearrange("p n (w f) -> p n w f", w=2).unsqueeze(3).to_broadcast(shape),
-                in1=table[:, rows].rearrange("p n a h i -> p n a (h i)").unsqueeze(2).to_broadcast(shape),
-                op=ALU.mult,
-            )
-
-        def add_and_store(b):
-            products = products_tiles[b]
+        def rotate(b):
+            products = products_pool.tile([P, ROWS, 2, 2, HEAD], F32)
+            for o in range(BANKS):
+                rows = slice(TILES_PER_BANK * o, TILES_PER_BANK * (o + 1))
+                shape = [P, TILES_PER_BANK, 2, 2, HEAD]
+                nc.vector.tensor_tensor(
+                    out=products[:, rows],
+                    in0=sums_tiles[b][o][:].rearrange("p n (w f) -> p n w f", w=2).unsqueeze(3).to_broadcast(shape),
+                    in1=table[:, rows].rearrange("p n a h i -> p n a (h i)").unsqueeze(2).to_broadcast(shape),
+                    op=ALU.mult,
+                )
             rotated = rotated_pool.tile([P, 2, ROWS, HEAD], F32)
-            nc.gpsimd.tensor_tensor(
-                out=rotated[:].rearrange("p w r (i h) -> p r w i h", h=2),
-                in0=products[:, :, :, :, 0:PAIRS].rearrange("p r w h i -> p r w i h"),
-                in1=products[:, :, :, :, PAIRS:HEAD].rearrange("p r w h i -> p r w i h"),
-                op=ALU.add,
-            )
+            for o, adder in enumerate((nc.vector, nc.gpsimd)):
+                rows = slice(TILES_PER_BANK * o, TILES_PER_BANK * (o + 1))
+                adder.tensor_tensor(
+                    out=rotated[:, :, rows, :].rearrange("p w n (i h) -> p n w i h", h=2),
+                    in0=products[:, rows, :, :, 0:PAIRS].rearrange("p n w h i -> p n w i h"),
+                    in1=products[:, rows, :, :, PAIRS:HEAD].rearrange("p n w h i -> p n w i h"),
+                    op=ALU.add,
+                )
             for w, out in enumerate((out_0, out_1)):
                 nc.sync.dma_start(
                     out=out[b].rearrange("(p r) f -> p (r f)", r=ROWS),
@@ -224,17 +219,13 @@ def tile_head_pa_kernel(tc, x, Wq, Wk, out_0, out_1):
         fill_rotation_table(nc, half, table)
 
         transpose(0)
-        transpose(1)
         quantise(0)
-        for unit in range(UNITS):
-            if unit + 2 < UNITS:
-                transpose(unit + 2)
-            project(unit)
-            if unit + 1 < UNITS:
-                quantise(unit + 1)
-            multiply(unit)
-            if unit % CHUNK_UNITS == CHUNK_UNITS - 1:
-                b = unit // CHUNK_UNITS
-                add_and_store(b)
-                if b + X_CHUNKS_IN_SBUF < BATCH:
-                    load(b + X_CHUNKS_IN_SBUF)
+        for b in range(BATCH):
+            if b + 1 < BATCH:
+                transpose(b + 1)
+            project(b)
+            if b + 1 < BATCH:
+                quantise(b + 1)
+            rotate(b)
+            if b + X_CHUNKS_IN_SBUF < BATCH:
+                load(b + X_CHUNKS_IN_SBUF)

@@ -71,15 +71,15 @@ def half_angle_squares(nc, pool):
 
 
 def fill_rotation_table(nc, half, table):
-    for row, column in ((0, 0), (1, 1)):
+    for h in range(2):
         nc.vector.tensor_scalar(
-            out=table[:, :, row, column, :], in0=half[:, 0], scalar1=-2.0, scalar2=1.0, op0=ALU.mult, op1=ALU.add
+            out=table[:, :, 0, :, h], in0=half[:, 0], scalar1=-2.0, scalar2=1.0, op0=ALU.mult, op1=ALU.add
         )
     nc.vector.tensor_scalar(
-        out=table[:, :, 0, 1, :], in0=half[:, 1], scalar1=-2.0, scalar2=1.0, op0=ALU.mult, op1=ALU.add
+        out=table[:, :, 1, :, 1], in0=half[:, 1], scalar1=-2.0, scalar2=1.0, op0=ALU.mult, op1=ALU.add
     )
     nc.vector.tensor_scalar(
-        out=table[:, :, 1, 0, :], in0=half[:, 1], scalar1=2.0, scalar2=-1.0, op0=ALU.mult, op1=ALU.add
+        out=table[:, :, 1, :, 0], in0=half[:, 1], scalar1=2.0, scalar2=-1.0, op0=ALU.mult, op1=ALU.add
     )
 
 
@@ -94,17 +94,17 @@ def load_weights(nc, pool, weights):
 
 
 def quantise_weights(nc, pool, w_rows, w_codes, w_scales):
-    w_grouped = pool.tile([P, PASSES, 2, 2, PAIRS, PACK], BF16, align_bytes=64)
+    w_grouped = pool.tile([P, PASSES, 2, HEAD, PACK], BF16, align_bytes=64)
     for g in range(PASSES):
         for w in range(2):
             nc.vector.tensor_copy(
                 out=w_grouped[:, g, w],
-                in_=w_rows[:, w, PACK * g : PACK * (g + 1), :].rearrange("p t (i h) -> p h i t", h=2),
+                in_=w_rows[:, w, PACK * g : PACK * (g + 1), :].rearrange("p t f -> p f t"),
             )
     nc.vector.quantize_mx(
         out=w_codes[:].bitcast(FP8X4),
         scales=w_scales[:],
-        in_=w_grouped[:].rearrange("p g w h i t -> p (g w h i t)"),
+        in_=w_grouped[:].rearrange("p g w f t -> p (g w f t)"),
     )
 
 
@@ -187,18 +187,16 @@ def tile_head_pa_kernel(tc, x, Wq, Wk, out_0, out_1):
                 nc.vector.tensor_tensor(
                     out=products[:, rows],
                     in0=sums_tiles[b][o][:].rearrange("p n (w f) -> p n w f", w=2).unsqueeze(3).to_broadcast(shape),
-                    in1=table[:, rows].rearrange("p n a h i -> p n a (h i)").unsqueeze(2).to_broadcast(shape),
+                    in1=table[:, rows].rearrange("p n a i h -> p n a (i h)").unsqueeze(2).to_broadcast(shape),
                     op=ALU.mult,
                 )
             rotated = rotated_pool.tile([P, 2, ROWS, HEAD], F32)
-            for o, adder in enumerate((nc.vector, nc.gpsimd)):
-                rows = slice(TILES_PER_BANK * o, TILES_PER_BANK * (o + 1))
-                adder.tensor_tensor(
-                    out=rotated[:, :, rows, :].rearrange("p w n (i h) -> p n w i h", h=2),
-                    in0=products[:, rows, :, :, 0:PAIRS].rearrange("p n w h i -> p n w i h"),
-                    in1=products[:, rows, :, :, PAIRS:HEAD].rearrange("p n w h i -> p n w i h"),
-                    op=ALU.add,
-                )
+            nc.gpsimd.tensor_tensor(
+                out=rotated[:].rearrange("p w r (i h) -> p r w i h", h=2),
+                in0=products[:, :, :, 0, :].rearrange("p r w (i h) -> p r w i h", h=2),
+                in1=products[:, :, :, 1, :].rearrange("p r w (i h) -> p r w i h", h=2)[:, :, :, :, ::-1],
+                op=ALU.add,
+            )
             for w, out in enumerate((out_0, out_1)):
                 nc.sync.dma_start(
                     out=out[b].rearrange("(p r) f -> p (r f)", r=ROWS),
@@ -207,7 +205,7 @@ def tile_head_pa_kernel(tc, x, Wq, Wk, out_0, out_1):
 
         w_codes = const.tile([P, PASSES * FEATURES], U32, align_bytes=64)
         w_scales = const.tile([P, PASSES * FEATURES], U8, align_bytes=64)
-        table = const.tile([P, ROWS, 2, 2, PAIRS], F32)
+        table = const.tile([P, ROWS, 2, PAIRS, 2], F32)
         identity = const.tile([P, P], F32)
 
         w_rows = load_weights(nc, const, (Wq, Wk))

@@ -23,6 +23,7 @@ WORDS = CHANNELS // 2
 TILE_COLS = PASSES * P
 TILES_PER_BANK = 2
 BANKS = ROWS // TILES_PER_BANK
+BANK_COLS = TILES_PER_BANK * TILE_COLS
 X_CHUNKS_IN_SBUF = 8
 
 FLOPS = 2 * BATCH * TOKENS * CHANNELS * FEATURES
@@ -31,7 +32,7 @@ RATIO = 10000.0 ** (-2.0 / PAIRS)
 ROUND_TO_WHOLE = 1.5 * 2**23
 
 
-def half_angle_squares(nc, pool):
+def half_angle_sines(nc, pool):
     position = pool.tile([P, ROWS], F32)
     nc.gpsimd.iota(
         position[:],
@@ -40,53 +41,60 @@ def half_angle_squares(nc, pool):
         channel_multiplier=ROWS,
         allow_small_or_imprecise_dtypes=True,
     )
-    powers = pool.tile([P, PAIRS], F32)
-    nc.vector.memset(powers[:, 0:1], 1.0)
-    filled = 1
-    while filled < PAIRS:
-        nc.vector.tensor_scalar_mul(
-            out=powers[:, filled : 2 * filled], in0=powers[:, 0:filled], scalar1=RATIO**filled
-        )
-        filled *= 2
-    shape = [P, ROWS, PAIRS]
-    turns = pool.tile(shape, F32)
-    nc.vector.scalar_tensor_tensor(
-        out=turns[:],
-        in0=powers[:].unsqueeze(1).to_broadcast(shape),
-        scalar=1.0 / (RATIO * 2.0 * math.pi),
-        in1=position[:].unsqueeze(2).to_broadcast(shape),
+    ones = pool.tile([P, PAIRS], F32)
+    nc.vector.memset(ones[:], 1.0)
+    ratio = pool.tile([P, PAIRS], F32)
+    nc.vector.tensor_scalar_mul(out=ratio[:], in0=ones[:], scalar1=RATIO)
+    turns_per_token = pool.tile([P, PAIRS], F32)
+    nc.vector.tensor_tensor_scan(
+        out=turns_per_token[:],
+        data0=ratio[:],
+        data1=ones[:],
+        initial=RATIO**-2 / (2.0 * math.pi),
         op0=ALU.mult,
         op1=ALU.mult,
     )
+    shape = [P, ROWS, PAIRS]
+    turns = pool.tile(shape, F32)
+    nc.vector.tensor_tensor(
+        out=turns[:],
+        in0=turns_per_token[:].unsqueeze(1).to_broadcast(shape),
+        in1=position[:].unsqueeze(2).to_broadcast(shape),
+        op=ALU.mult,
+    )
     whole = pool.tile(shape, F32)
     nc.vector.tensor_scalar_add(out=whole[:], in0=turns[:], scalar1=ROUND_TO_WHOLE)
-    half = pool.tile([P, 2, ROWS, PAIRS], F32)
+    minus = pool.tile(shape, F32)
     nc.vector.scalar_tensor_tensor(
-        out=half[:, 0], in0=whole[:], scalar=ROUND_TO_WHOLE, in1=turns[:], op0=ALU.subtract, op1=ALU.subtract
+        out=minus[:], in0=whole[:], scalar=ROUND_TO_WHOLE, in1=turns[:], op0=ALU.subtract, op1=ALU.subtract
     )
-    nc.vector.tensor_scalar_add(out=half[:, 1], in0=half[:, 0], scalar1=0.25)
-    nc.scalar.activation(out=half[:], in_=half[:], func=ACT.Sin, scale=math.pi)
-    nc.scalar.activation(out=half[:], in_=half[:], func=ACT.Square)
+    half = pool.tile([P, 2, ROWS, PAIRS], F32)
+    nc.scalar.activation(out=half[:, 0], in_=minus[:], func=ACT.Sin, scale=math.pi)
+    nc.scalar.activation(out=half[:, 1], in_=minus[:], func=ACT.Sin, scale=math.pi, bias=math.pi / 4.0)
     return half
 
 
-def fill_rotation_table(nc, half, table):
-    for h in range(2):
-        nc.vector.tensor_scalar(
-            out=table[:, :, 0, :, h], in0=half[:, 0], scalar1=-2.0, scalar2=1.0, op0=ALU.mult, op1=ALU.add
-        )
+def fill_rotation_table(nc, squares, table):
     nc.vector.tensor_scalar(
-        out=table[:, :, 1, :, 1], in0=half[:, 1], scalar1=-2.0, scalar2=1.0, op0=ALU.mult, op1=ALU.add
+        out=table[:, :, 0],
+        in0=squares[:, 0].unsqueeze(3).to_broadcast([P, ROWS, PAIRS, 2]),
+        scalar1=-2.0,
+        scalar2=1.0,
+        op0=ALU.mult,
+        op1=ALU.add,
     )
     nc.vector.tensor_scalar(
-        out=table[:, :, 1, :, 0], in0=half[:, 1], scalar1=2.0, scalar2=-1.0, op0=ALU.mult, op1=ALU.add
+        out=table[:, :, 1, :, 1], in0=squares[:, 1], scalar1=-2.0, scalar2=1.0, op0=ALU.mult, op1=ALU.add
+    )
+    nc.vector.tensor_scalar(
+        out=table[:, :, 1, :, 0], in0=squares[:, 1], scalar1=2.0, scalar2=-1.0, op0=ALU.mult, op1=ALU.add
     )
 
 
 def load_weights(nc, pool, weights):
     w_rows = pool.tile([P, 2, PASSES * PACK, HEAD], BF16)
     for w, weight in enumerate(weights):
-        nc.scalar.dma_start(
+        nc.sync.dma_start(
             out=w_rows[:, w].rearrange("p (c e) f -> p c (e f)", e=2),
             in_=weight.rearrange("(c p e) f -> p c (e f)", p=P, e=2),
         )
@@ -116,7 +124,7 @@ def tile_head_pa_kernel(tc, x, Wq, Wk, out_0, out_1):
         x_pool = ctx.enter_context(tc.tile_pool(name="x", bufs=X_CHUNKS_IN_SBUF))
         grouped_pool = ctx.enter_context(tc.tile_pool(name="grouped", bufs=3))
         codes_pool = ctx.enter_context(tc.tile_pool(name="codes", bufs=3))
-        products_pool = ctx.enter_context(tc.tile_pool(name="products", bufs=3))
+        products_pool = ctx.enter_context(tc.tile_pool(name="products", bufs=6))
         rotated_pool = ctx.enter_context(tc.tile_pool(name="rotated", bufs=4))
         transposed_pool = ctx.enter_context(tc.psum_pool(name="transposed", bufs=ROWS))
         sums_pool = ctx.enter_context(tc.psum_pool(name="sums", bufs=2 * BANKS))
@@ -125,10 +133,11 @@ def tile_head_pa_kernel(tc, x, Wq, Wk, out_0, out_1):
         grouped_tiles = {}
         codes_tiles = {}
         sums_tiles = {}
+        rotated_tiles = {}
 
         def load(b):
             x_rows = x_pool.tile([P, ROWS * CHANNELS], BF16)
-            pieces = ROWS if b == 0 else 1
+            pieces = ROWS if b < 2 else 1
             width = ROWS * CHANNELS // pieces
             for piece in range(pieces):
                 columns = slice(width * piece, width * (piece + 1))
@@ -137,11 +146,13 @@ def tile_head_pa_kernel(tc, x, Wq, Wk, out_0, out_1):
                 )
             x_tiles[b] = x_rows
 
-        def transpose(b):
+        def transpose(b, tiles=range(ROWS)):
             x_words = x_tiles[b][:].bitcast(F32)
-            grouped = grouped_pool.tile([P, ROWS * TILE_COLS * PACK], BF16, align_bytes=64)
-            grouped_words = grouped[:].bitcast(F32)
-            for r in range(ROWS):
+            if b not in grouped_tiles:
+                grouped = grouped_pool.tile([P, ROWS * TILE_COLS * PACK], BF16, align_bytes=64)
+                grouped_tiles[b] = grouped
+            grouped_words = grouped_tiles[b][:].bitcast(F32)
+            for r in tiles:
                 transposed = transposed_pool.tile([P, WORDS // P, P], F32)
                 for j in range(WORDS // P):
                     first = WORDS * r + P * j
@@ -152,18 +163,23 @@ def tile_head_pa_kernel(tc, x, Wq, Wk, out_0, out_1):
                     ),
                     in_=transposed[:].rearrange("p (g u) c -> p g c u", u=2),
                 )
-            grouped_tiles[b] = grouped
 
-        def quantise(b):
-            codes = codes_pool.tile([P, ROWS * TILE_COLS], U32, align_bytes=64)
-            scales = codes_pool.tile([P, ROWS * TILE_COLS], U8, align_bytes=64)
-            nc.vector.quantize_mx(out=codes[:].bitcast(FP8X4), scales=scales[:], in_=grouped_tiles[b][:])
-            codes_tiles[b] = (codes, scales)
-
-        def project(b):
+        def quantise(b, banks):
+            if b not in codes_tiles:
+                codes = codes_pool.tile([P, ROWS * TILE_COLS], U32, align_bytes=64)
+                scales = codes_pool.tile([P, ROWS * TILE_COLS], U8, align_bytes=64)
+                codes_tiles[b] = (codes, scales)
             codes, scales = codes_tiles[b]
-            sums_tiles[b] = []
-            for o in range(BANKS):
+            columns = slice(BANK_COLS * banks.start, BANK_COLS * banks.stop)
+            nc.vector.quantize_mx(
+                out=codes[:, columns].bitcast(FP8X4),
+                scales=scales[:, columns],
+                in_=grouped_tiles[b][:, PACK * columns.start : PACK * columns.stop],
+            )
+
+        def project(b, banks):
+            codes, scales = codes_tiles[b]
+            for o in banks:
                 sums = sums_pool.tile([P, TILES_PER_BANK, FEATURES], F32)
                 for n in range(TILES_PER_BANK):
                     for g in range(PASSES):
@@ -177,31 +193,36 @@ def tile_head_pa_kernel(tc, x, Wq, Wk, out_0, out_1):
                             start=(g == 0),
                             stop=(g == PASSES - 1),
                         )
-                sums_tiles[b].append(sums)
+                sums_tiles[b, o] = sums
 
-        def rotate(b):
-            products = products_pool.tile([P, ROWS, 2, 2, HEAD], F32)
-            for o in range(BANKS):
-                rows = slice(TILES_PER_BANK * o, TILES_PER_BANK * (o + 1))
-                shape = [P, TILES_PER_BANK, 2, 2, HEAD]
-                nc.vector.tensor_tensor(
-                    out=products[:, rows],
-                    in0=sums_tiles[b][o][:].rearrange("p n (w f) -> p n w f", w=2).unsqueeze(3).to_broadcast(shape),
-                    in1=table[:, rows].rearrange("p n a i h -> p n a (i h)").unsqueeze(2).to_broadcast(shape),
-                    op=ALU.mult,
-                )
-            rotated = rotated_pool.tile([P, 2, ROWS, HEAD], F32)
-            nc.gpsimd.tensor_tensor(
-                out=rotated[:].rearrange("p w r (i h) -> p r w i h", h=2),
-                in0=products[:, :, :, 0, :].rearrange("p r w (i h) -> p r w i h", h=2),
-                in1=products[:, :, :, 1, :].rearrange("p r w (i h) -> p r w i h", h=2)[:, :, :, :, ::-1],
+        def rotate(b, o, adder):
+            products = products_pool.tile([P, TILES_PER_BANK, 2, 2, HEAD], F32)
+            rows = slice(TILES_PER_BANK * o, TILES_PER_BANK * (o + 1))
+            shape = [P, TILES_PER_BANK, 2, 2, HEAD]
+            nc.vector.tensor_tensor(
+                out=products[:],
+                in0=sums_tiles[b, o][:].rearrange("p n (w f) -> p n w f", w=2).unsqueeze(3).to_broadcast(shape),
+                in1=table[:, rows].rearrange("p n a i h -> p n a (i h)").unsqueeze(2).to_broadcast(shape),
+                op=ALU.mult,
+            )
+            if b not in rotated_tiles:
+                rotated = rotated_pool.tile([P, 2, ROWS, HEAD], F32)
+                rotated_tiles[b] = rotated
+            adder.tensor_tensor(
+                out=rotated_tiles[b][:, :, rows].rearrange("p w n (i h) -> p n w i h", h=2),
+                in0=products[:, :, :, 0, :].rearrange("p n w (i h) -> p n w i h", h=2),
+                in1=products[:, :, :, 1, :].rearrange("p n w (i h) -> p n w i h", h=2)[:, :, :, :, ::-1],
                 op=ALU.add,
             )
+
+        def store(b):
             for w, out in enumerate((out_0, out_1)):
                 nc.sync.dma_start(
                     out=out[b].rearrange("(p r) f -> p (r f)", r=ROWS),
-                    in_=rotated[:, w].rearrange("p r f -> p (r f)"),
+                    in_=rotated_tiles[b][:, w].rearrange("p r f -> p (r f)"),
                 )
+            if b + X_CHUNKS_IN_SBUF < BATCH:
+                load(b + X_CHUNKS_IN_SBUF)
 
         w_codes = const.tile([P, PASSES * FEATURES], U32, align_bytes=64)
         w_scales = const.tile([P, PASSES * FEATURES], U8, align_bytes=64)
@@ -211,19 +232,39 @@ def tile_head_pa_kernel(tc, x, Wq, Wk, out_0, out_1):
         w_rows = load_weights(nc, const, (Wq, Wk))
         for b in range(X_CHUNKS_IN_SBUF):
             load(b)
-        half = half_angle_squares(nc, const)
+        half = half_angle_sines(nc, const)
         make_identity(nc, identity[:])
         quantise_weights(nc, const, w_rows, w_codes, w_scales)
-        fill_rotation_table(nc, half, table)
 
-        transpose(0)
-        quantise(0)
-        for b in range(BATCH):
+        first, second = range(0, 1), range(1, 2)
+        both = range(0, 2)
+        transpose(0, (0, 1))
+        nc.scalar.activation(out=half[:], in_=half[:], func=ACT.Square)
+        transpose(0, (2, 3))
+        quantise(0, first)
+        fill_rotation_table(nc, half, table)
+        quantise(0, second)
+        transpose(1, (0, 1))
+        project(0, first)
+        transpose(1, (2, 3))
+        project(0, second)
+        rotate(0, 0, nc.gpsimd)
+        quantise(1, first)
+        rotate(0, 1, nc.gpsimd)
+        store(0)
+        quantise(1, second)
+        transpose(2)
+        project(1, both)
+        rotate(1, 0, nc.gpsimd)
+        quantise(2, both)
+        rotate(1, 1, nc.gpsimd)
+        store(1)
+        for b in range(2, BATCH):
             if b + 1 < BATCH:
                 transpose(b + 1)
-            project(b)
+            project(b, both)
             if b + 1 < BATCH:
-                quantise(b + 1)
-            rotate(b)
-            if b + X_CHUNKS_IN_SBUF < BATCH:
-                load(b + X_CHUNKS_IN_SBUF)
+                quantise(b + 1, both)
+            rotate(b, 0, nc.gpsimd)
+            rotate(b, 1, nc.vector if b + 1 == BATCH else nc.gpsimd)
+            store(b)

@@ -24,6 +24,8 @@ TILE_COLS = PASSES * P
 TILES_PER_BANK = 2
 BANKS = ROWS // TILES_PER_BANK
 BANK_COLS = TILES_PER_BANK * TILE_COLS
+LAST = ROWS - 1
+ANGLES = LAST * PAIRS + P
 X_CHUNKS_IN_SBUF = 8
 
 FLOPS = 2 * BATCH * TOKENS * CHANNELS * FEATURES
@@ -32,62 +34,75 @@ RATIO = 10000.0 ** (-2.0 / PAIRS)
 ROUND_TO_WHOLE = 1.5 * 2**23
 
 
-def half_angle_sines(nc, pool):
-    position = pool.tile([P, ROWS], F32)
-    nc.gpsimd.iota(
-        position[:],
-        pattern=[[1, ROWS]],
-        base=0,
-        channel_multiplier=ROWS,
-        allow_small_or_imprecise_dtypes=True,
-    )
-    ones = pool.tile([P, PAIRS], F32)
-    nc.vector.memset(ones[:], 1.0)
-    ratio = pool.tile([P, PAIRS], F32)
-    nc.vector.tensor_scalar_mul(out=ratio[:], in0=ones[:], scalar1=RATIO)
-    turns_per_token = pool.tile([P, PAIRS], F32)
+def signed_turns(nc, pool):
+    minus_ones = pool.tile([P, PAIRS, 2], F32)
+    nc.vector.memset(minus_ones[:], -1.0)
+    factors = pool.tile([P, PAIRS, 2], F32)
+    nc.vector.memset(factors[:], 1.0)
+    nc.vector.tensor_scalar_mul(out=factors[:, :, 0], in0=minus_ones[:, :, 0], scalar1=-RATIO)
+    signed = pool.tile([P, PAIRS, 2], F32)
     nc.vector.tensor_tensor_scan(
-        out=turns_per_token[:],
-        data0=ratio[:],
-        data1=ones[:],
+        out=signed[:].rearrange("p i h -> p (i h)"),
+        data0=factors[:].rearrange("p i h -> p (i h)"),
+        data1=minus_ones[:].rearrange("p i h -> p (i h)"),
         initial=RATIO**-2 / (2.0 * math.pi),
         op0=ALU.mult,
         op1=ALU.mult,
     )
-    shape = [P, ROWS, PAIRS]
-    turns = pool.tile(shape, F32)
+    return signed
+
+
+def half_angle_sines(nc, pool, signed, signed_by_feature):
+    position = pool.tile([P, LAST], F32)
+    nc.gpsimd.iota(
+        position[:], pattern=[[1, LAST]], base=0, channel_multiplier=ROWS, allow_small_or_imprecise_dtypes=True
+    )
+    position_last = pool.tile([P, P], F32)
+    nc.gpsimd.iota(
+        position_last[:], pattern=[[ROWS, P]], base=LAST, channel_multiplier=0, allow_small_or_imprecise_dtypes=True
+    )
+    shape = [P, LAST, PAIRS]
+    turns = pool.tile([P, ANGLES], F32)
     nc.vector.tensor_tensor(
-        out=turns[:],
-        in0=turns_per_token[:].unsqueeze(1).to_broadcast(shape),
+        out=turns[:, 0 : LAST * PAIRS].rearrange("p (r i) -> p r i", r=LAST),
+        in0=signed[:, :, 1].unsqueeze(1).to_broadcast(shape),
         in1=position[:].unsqueeze(2).to_broadcast(shape),
         op=ALU.mult,
     )
-    whole = pool.tile(shape, F32)
+    nc.vector.tensor_tensor(
+        out=turns[:, LAST * PAIRS : ANGLES], in0=signed_by_feature, in1=position_last[:], op=ALU.mult
+    )
+    whole = pool.tile([P, ANGLES], F32)
     nc.vector.tensor_scalar_add(out=whole[:], in0=turns[:], scalar1=ROUND_TO_WHOLE)
-    minus = pool.tile(shape, F32)
+    minus = pool.tile([P, ANGLES], F32)
     nc.vector.scalar_tensor_tensor(
         out=minus[:], in0=whole[:], scalar=ROUND_TO_WHOLE, in1=turns[:], op0=ALU.subtract, op1=ALU.subtract
     )
-    half = pool.tile([P, 2, ROWS, PAIRS], F32)
+    half = pool.tile([P, 2, ANGLES], F32)
     nc.scalar.activation(out=half[:, 0], in_=minus[:], func=ACT.Sin, scale=math.pi)
     nc.scalar.activation(out=half[:, 1], in_=minus[:], func=ACT.Sin, scale=math.pi, bias=math.pi / 4.0)
     return half
 
 
 def fill_rotation_table(nc, squares, table):
+    by_token = squares[:, :, 0 : LAST * PAIRS].rearrange("p s (r i) -> p s r i", r=LAST)
+    pairs = table[:].rearrange("p r a (i h) -> p r a i h", h=2)
     nc.vector.tensor_scalar(
-        out=table[:, :, 0],
-        in0=squares[:, 0].unsqueeze(3).to_broadcast([P, ROWS, PAIRS, 2]),
+        out=pairs[:, 0:LAST, 0],
+        in0=by_token[:, 0].unsqueeze(3).to_broadcast([P, LAST, PAIRS, 2]),
         scalar1=-2.0,
         scalar2=1.0,
         op0=ALU.mult,
         op1=ALU.add,
     )
     nc.vector.tensor_scalar(
-        out=table[:, :, 1, :, 1], in0=squares[:, 1], scalar1=-2.0, scalar2=1.0, op0=ALU.mult, op1=ALU.add
+        out=pairs[:, 0:LAST, 1, :, 1], in0=by_token[:, 1], scalar1=-2.0, scalar2=1.0, op0=ALU.mult, op1=ALU.add
     )
     nc.vector.tensor_scalar(
-        out=table[:, :, 1, :, 0], in0=squares[:, 1], scalar1=2.0, scalar2=-1.0, op0=ALU.mult, op1=ALU.add
+        out=pairs[:, 0:LAST, 1, :, 0], in0=by_token[:, 1], scalar1=2.0, scalar2=-1.0, op0=ALU.mult, op1=ALU.add
+    )
+    nc.vector.tensor_scalar(
+        out=table[:, LAST], in0=squares[:, :, LAST * PAIRS : ANGLES], scalar1=-2.0, scalar2=1.0, op0=ALU.mult, op1=ALU.add
     )
 
 
@@ -122,17 +137,19 @@ def tile_head_pa_kernel(tc, x, Wq, Wk, out_0, out_1):
         ctx.enter_context(tc.manual_schedule())
         const = ctx.enter_context(tc.tile_pool(name="const", bufs=1))
         x_pool = ctx.enter_context(tc.tile_pool(name="x", bufs=X_CHUNKS_IN_SBUF))
-        grouped_pool = ctx.enter_context(tc.tile_pool(name="grouped", bufs=3))
-        codes_pool = ctx.enter_context(tc.tile_pool(name="codes", bufs=3))
-        products_pool = ctx.enter_context(tc.tile_pool(name="products", bufs=6))
+        grouped_pool = ctx.enter_context(tc.tile_pool(name="grouped", bufs=4))
+        codes_pool = ctx.enter_context(tc.tile_pool(name="codes", bufs=5))
+        products_pool = ctx.enter_context(tc.tile_pool(name="products", bufs=3))
         rotated_pool = ctx.enter_context(tc.tile_pool(name="rotated", bufs=4))
         transposed_pool = ctx.enter_context(tc.psum_pool(name="transposed", bufs=ROWS))
-        sums_pool = ctx.enter_context(tc.psum_pool(name="sums", bufs=2 * BANKS))
+        sums_pool = ctx.enter_context(tc.psum_pool(name="sums", bufs=3))
+        turned_pool = ctx.enter_context(tc.psum_pool(name="turned", bufs=1))
 
         x_tiles = {}
         grouped_tiles = {}
         codes_tiles = {}
         sums_tiles = {}
+        products_tiles = {}
         rotated_tiles = {}
 
         def load(b):
@@ -182,58 +199,101 @@ def tile_head_pa_kernel(tc, x, Wq, Wk, out_0, out_1):
             for o in banks:
                 sums = sums_pool.tile([P, TILES_PER_BANK, FEATURES], F32)
                 for n in range(TILES_PER_BANK):
-                    for g in range(PASSES):
-                        first = TILE_COLS * (TILES_PER_BANK * o + n) + P * g
-                        nc.tensor.matmul_mx(
-                            out=sums[:, n, :],
-                            lhsT=codes[:, first : first + P].bitcast(FP8X4),
-                            lhsT_scale=scales[:, first : first + P],
-                            rhs=w_codes[:, FEATURES * g : FEATURES * (g + 1)].bitcast(FP8X4),
-                            rhs_scale=w_scales[:, FEATURES * g : FEATURES * (g + 1)],
-                            start=(g == 0),
-                            stop=(g == PASSES - 1),
-                        )
+                    r = TILES_PER_BANK * o + n
+                    for w in (0, 1) if r == LAST else (0,):
+                        for g in range(PASSES):
+                            tokens = slice(TILE_COLS * r + P * g, TILE_COLS * r + P * (g + 1))
+                            if r == LAST:
+                                features = slice(FEATURES * g + HEAD * w, FEATURES * g + HEAD * (w + 1))
+                                columns = slice(HEAD * w, HEAD * (w + 1))
+                                left, right = (w_codes, w_scales, features), (codes, scales, tokens)
+                            else:
+                                features = slice(FEATURES * g, FEATURES * (g + 1))
+                                columns = slice(0, FEATURES)
+                                left, right = (codes, scales, tokens), (w_codes, w_scales, features)
+                            nc.tensor.matmul_mx(
+                                out=sums[:, n, columns],
+                                lhsT=left[0][:, left[2]].bitcast(FP8X4),
+                                lhsT_scale=left[1][:, left[2]],
+                                rhs=right[0][:, right[2]].bitcast(FP8X4),
+                                rhs_scale=right[1][:, right[2]],
+                                start=(g == 0),
+                                stop=(g == PASSES - 1),
+                            )
                 sums_tiles[b, o] = sums
 
-        def rotate(b, o, adder):
-            products = products_pool.tile([P, TILES_PER_BANK, 2, 2, HEAD], F32)
+        def multiply(b, o):
+            if o == 0:
+                products = products_pool.tile([P, ROWS, 2, 2, HEAD], F32)
+                products_tiles[b] = products
             rows = slice(TILES_PER_BANK * o, TILES_PER_BANK * (o + 1))
             shape = [P, TILES_PER_BANK, 2, 2, HEAD]
             nc.vector.tensor_tensor(
-                out=products[:],
+                out=products_tiles[b][:, rows],
                 in0=sums_tiles[b, o][:].rearrange("p n (w f) -> p n w f", w=2).unsqueeze(3).to_broadcast(shape),
-                in1=table[:, rows].rearrange("p n a i h -> p n a (i h)").unsqueeze(2).to_broadcast(shape),
+                in1=table[:, rows].unsqueeze(2).to_broadcast(shape),
                 op=ALU.mult,
             )
+
+        def add(b, weights, adder):
             if b not in rotated_tiles:
                 rotated = rotated_pool.tile([P, 2, ROWS, HEAD], F32)
                 rotated_tiles[b] = rotated
+            products = products_tiles[b][:, 0:LAST, weights].rearrange("p r w a (i h) -> p r w a i h", h=2)
             adder.tensor_tensor(
-                out=rotated_tiles[b][:, :, rows].rearrange("p w n (i h) -> p n w i h", h=2),
-                in0=products[:, :, :, 0, :].rearrange("p n w (i h) -> p n w i h", h=2),
-                in1=products[:, :, :, 1, :].rearrange("p n w (i h) -> p n w i h", h=2)[:, :, :, :, ::-1],
+                out=rotated_tiles[b][:, weights, 0:LAST].rearrange("p w r (i h) -> p r w i h", h=2),
+                in0=products[:, :, :, 0],
+                in1=products[:, :, :, 1, :, ::-1],
                 op=ALU.add,
             )
 
-        def store(b):
+        def add_last_tile(b):
+            turned = turned_pool.tile([P, 2, HEAD], F32)
+            for w in range(2):
+                for a, order in enumerate((identity, swap)):
+                    nc.tensor.matmul(
+                        turned[:, w, :],
+                        lhsT=products_tiles[b][:, LAST, w, a, :],
+                        rhs=order[:],
+                        start=(a == 0),
+                        stop=(a == 1),
+                        is_transpose=True,
+                    )
+            nc.scalar.copy(out=rotated_tiles[b][:, :, LAST, :], in_=turned[:])
+
+        def store(b, w, out):
+            nc.sync.dma_start(
+                out=out[b].rearrange("(p r) f -> p (r f)", r=ROWS),
+                in_=rotated_tiles[b][:, w].rearrange("p r f -> p (r f)"),
+            )
+
+        def finish(b):
+            add(b, slice(0, 2), nc.gpsimd)
+
+        def finish_store(b):
+            add_last_tile(b)
             for w, out in enumerate((out_0, out_1)):
-                nc.sync.dma_start(
-                    out=out[b].rearrange("(p r) f -> p (r f)", r=ROWS),
-                    in_=rotated_tiles[b][:, w].rearrange("p r f -> p (r f)"),
-                )
+                store(b, w, out)
             if b + X_CHUNKS_IN_SBUF < BATCH:
                 load(b + X_CHUNKS_IN_SBUF)
 
         w_codes = const.tile([P, PASSES * FEATURES], U32, align_bytes=64)
         w_scales = const.tile([P, PASSES * FEATURES], U8, align_bytes=64)
-        table = const.tile([P, ROWS, 2, PAIRS, 2], F32)
+        table = const.tile([P, ROWS, 2, HEAD], F32)
         identity = const.tile([P, P], F32)
+        swap = const.tile([P, P], F32)
 
         w_rows = load_weights(nc, const, (Wq, Wk))
         for b in range(X_CHUNKS_IN_SBUF):
             load(b)
-        half = half_angle_sines(nc, const)
+        signed = signed_turns(nc, const)
         make_identity(nc, identity[:])
+        nc.gpsimd.tensor_copy(
+            out=swap[:].rearrange("p (i h) -> p i h", h=2), in_=identity[:].rearrange("p (i h) -> p i h", h=2)[:, :, ::-1]
+        )
+        signed_by_feature = turned_pool.tile([P, 2, HEAD], F32, name="turned")
+        nc.tensor.transpose(signed_by_feature[:, 0, :], signed[:].rearrange("p i h -> p (i h)"), identity[:])
+        half = half_angle_sines(nc, const, signed, signed_by_feature[:, 0, :])
         quantise_weights(nc, const, w_rows, w_codes, w_scales)
 
         first, second = range(0, 1), range(1, 2)
@@ -248,23 +308,38 @@ def tile_head_pa_kernel(tc, x, Wq, Wk, out_0, out_1):
         project(0, first)
         transpose(1, (2, 3))
         project(0, second)
-        rotate(0, 0, nc.gpsimd)
+        multiply(0, 0)
         quantise(1, first)
-        rotate(0, 1, nc.gpsimd)
-        store(0)
+        multiply(0, 1)
+        finish(0)
         quantise(1, second)
         transpose(2)
         project(1, both)
-        rotate(1, 0, nc.gpsimd)
+        multiply(1, 0)
+        multiply(1, 1)
         quantise(2, both)
-        rotate(1, 1, nc.gpsimd)
-        store(1)
+        finish(1)
+        transpose(3)
+        finish_store(0)
+        project(2, both)
+        quantise(3, both)
         for b in range(2, BATCH):
-            if b + 1 < BATCH:
-                transpose(b + 1)
-            project(b, both)
-            if b + 1 < BATCH:
-                quantise(b + 1, both)
-            rotate(b, 0, nc.gpsimd)
-            rotate(b, 1, nc.vector if b + 1 == BATCH else nc.gpsimd)
-            store(b)
+            multiply(b, 0)
+            multiply(b, 1)
+            if b + 2 < BATCH:
+                transpose(b + 2)
+                finish_store(b - 1)
+                project(b + 1, both)
+                quantise(b + 2, both)
+                finish(b)
+            elif b + 1 < BATCH:
+                finish_store(b - 1)
+                project(b + 1, both)
+                finish(b)
+            else:
+                finish_store(b - 1)
+                for w, out in enumerate((out_0, out_1)):
+                    add(b, slice(w, w + 1), nc.vector)
+                add_last_tile(b)
+                for w, out in enumerate((out_0, out_1)):
+                    store(b, w, out)

@@ -52,7 +52,7 @@ def signed_turns(nc, pool):
     return signed
 
 
-def half_angle_sines(nc, pool, signed, signed_by_feature):
+def minus_turns(nc, pool, signed, signed_by_feature):
     position = pool.tile([P, LAST], F32)
     nc.gpsimd.iota(
         position[:], pattern=[[1, LAST]], base=0, channel_multiplier=ROWS, allow_small_or_imprecise_dtypes=True
@@ -78,6 +78,10 @@ def half_angle_sines(nc, pool, signed, signed_by_feature):
     nc.vector.scalar_tensor_tensor(
         out=minus[:], in0=whole[:], scalar=ROUND_TO_WHOLE, in1=turns[:], op0=ALU.subtract, op1=ALU.subtract
     )
+    return minus
+
+
+def half_angle_sines(nc, pool, minus):
     half = pool.tile([P, 2, ANGLES], F32)
     nc.scalar.activation(out=half[:, 0], in_=minus[:], func=ACT.Sin, scale=math.pi)
     nc.scalar.activation(out=half[:, 1], in_=minus[:], func=ACT.Sin, scale=math.pi, bias=math.pi / 4.0)
@@ -101,8 +105,8 @@ def fill_rotation_table(nc, squares, table):
     nc.vector.tensor_scalar(
         out=pairs[:, 0:LAST, 1, :, 0], in0=by_token[:, 1], scalar1=2.0, scalar2=-1.0, op0=ALU.mult, op1=ALU.add
     )
-    nc.vector.tensor_scalar(
-        out=table[:, LAST], in0=squares[:, :, LAST * PAIRS : ANGLES], scalar1=-2.0, scalar2=1.0, op0=ALU.mult, op1=ALU.add
+    nc.scalar.activation(
+        out=table[:, LAST], in_=squares[:, :, LAST * PAIRS : ANGLES], func=ACT.Identity, scale=-2.0, bias=1.0
     )
 
 
@@ -116,19 +120,17 @@ def load_weights(nc, pool, weights):
     return w_rows
 
 
-def quantise_weights(nc, pool, w_rows, w_codes, w_scales):
+def group_weights(nc, pool, w_rows):
     w_grouped = pool.tile([P, PASSES, 2, HEAD, PACK], BF16, align_bytes=64)
     for g in range(PASSES):
-        for w in range(2):
-            nc.vector.tensor_copy(
-                out=w_grouped[:, g, w],
-                in_=w_rows[:, w, PACK * g : PACK * (g + 1), :].rearrange("p t f -> p f t"),
-            )
-    nc.vector.quantize_mx(
-        out=w_codes[:].bitcast(FP8X4),
-        scales=w_scales[:],
-        in_=w_grouped[:].rearrange("p g w f t -> p (g w f t)"),
-    )
+        q_rows, k_rows = (
+            w_rows[:, w, PACK * g : PACK * (g + 1), :].rearrange("p t f -> p f t") for w in range(2)
+        )
+        nc.gpsimd.tensor_scalar(
+            out=w_grouped[:, g, 0], in0=q_rows, scalar1=1.0, scalar2=0.0, op0=ALU.mult, op1=ALU.add
+        )
+        nc.vector.tensor_copy(out=w_grouped[:, g, 1], in_=k_rows)
+    return w_grouped
 
 
 def tile_head_pa_kernel(tc, x, Wq, Wk, out_0, out_1):
@@ -137,7 +139,7 @@ def tile_head_pa_kernel(tc, x, Wq, Wk, out_0, out_1):
         ctx.enter_context(tc.manual_schedule())
         const = ctx.enter_context(tc.tile_pool(name="const", bufs=1))
         x_pool = ctx.enter_context(tc.tile_pool(name="x", bufs=X_CHUNKS_IN_SBUF))
-        grouped_pool = ctx.enter_context(tc.tile_pool(name="grouped", bufs=4))
+        grouped_pool = ctx.enter_context(tc.tile_pool(name="grouped", bufs=5))
         codes_pool = ctx.enter_context(tc.tile_pool(name="codes", bufs=5))
         products_pool = ctx.enter_context(tc.tile_pool(name="products", bufs=3))
         rotated_pool = ctx.enter_context(tc.tile_pool(name="rotated", bufs=4))
@@ -151,17 +153,16 @@ def tile_head_pa_kernel(tc, x, Wq, Wk, out_0, out_1):
         sums_tiles = {}
         products_tiles = {}
         rotated_tiles = {}
+        end_tiles = {}
 
-        def load(b):
-            x_rows = x_pool.tile([P, ROWS * CHANNELS], BF16)
-            pieces = ROWS if b < 2 else 1
-            width = ROWS * CHANNELS // pieces
-            for piece in range(pieces):
-                columns = slice(width * piece, width * (piece + 1))
-                nc.sync.dma_start(
-                    out=x_rows[:, columns], in_=x[b].rearrange("(p r) k -> p (r k)", r=ROWS)[:, columns]
-                )
-            x_tiles[b] = x_rows
+        def load(b, tiles=slice(0, ROWS)):
+            if b not in x_tiles:
+                x_rows = x_pool.tile([P, ROWS * CHANNELS], BF16)
+                x_tiles[b] = x_rows
+            columns = slice(CHANNELS * tiles.start, CHANNELS * tiles.stop)
+            nc.sync.dma_start(
+                out=x_tiles[b][:, columns], in_=x[b].rearrange("(p r) k -> p (r k)", r=ROWS)[:, columns]
+            )
 
         def transpose(b, tiles=range(ROWS)):
             x_words = x_tiles[b][:].bitcast(F32)
@@ -222,15 +223,16 @@ def tile_head_pa_kernel(tc, x, Wq, Wk, out_0, out_1):
                             )
                 sums_tiles[b, o] = sums
 
-        def multiply(b, o):
-            if o == 0:
+        def multiply(b, o, weights=slice(0, 2)):
+            if b not in products_tiles:
                 products = products_pool.tile([P, ROWS, 2, 2, HEAD], F32)
                 products_tiles[b] = products
             rows = slice(TILES_PER_BANK * o, TILES_PER_BANK * (o + 1))
-            shape = [P, TILES_PER_BANK, 2, 2, HEAD]
+            shape = [P, TILES_PER_BANK, weights.stop - weights.start, 2, HEAD]
+            sums = sums_tiles[b, o][:].rearrange("p n (w f) -> p n w f", w=2)[:, :, weights]
             nc.vector.tensor_tensor(
-                out=products_tiles[b][:, rows],
-                in0=sums_tiles[b, o][:].rearrange("p n (w f) -> p n w f", w=2).unsqueeze(3).to_broadcast(shape),
+                out=products_tiles[b][:, rows, weights],
+                in0=sums.unsqueeze(3).to_broadcast(shape),
                 in1=table[:, rows].unsqueeze(2).to_broadcast(shape),
                 op=ALU.mult,
             )
@@ -247,19 +249,18 @@ def tile_head_pa_kernel(tc, x, Wq, Wk, out_0, out_1):
                 op=ALU.add,
             )
 
-        def add_last_tile(b):
-            turned = turned_pool.tile([P, 2, HEAD], F32)
+        def add_last_tile(b, turned, rotated_last):
             for w in range(2):
                 for a, order in enumerate((identity, swap)):
                     nc.tensor.matmul(
-                        turned[:, w, :],
+                        turned[:, w, 0:HEAD],
                         lhsT=products_tiles[b][:, LAST, w, a, :],
                         rhs=order[:],
                         start=(a == 0),
                         stop=(a == 1),
                         is_transpose=True,
                     )
-            nc.scalar.copy(out=rotated_tiles[b][:, :, LAST, :], in_=turned[:])
+            nc.scalar.copy(out=rotated_last, in_=turned[:, :, 0:HEAD])
 
         def store(b, w, out):
             nc.sync.dma_start(
@@ -267,11 +268,23 @@ def tile_head_pa_kernel(tc, x, Wq, Wk, out_0, out_1):
                 in_=rotated_tiles[b][:, w].rearrange("p r f -> p (r f)"),
             )
 
+        def last_tile_end(b):
+            turned = sums_pool.tile([P, TILES_PER_BANK, FEATURES], F32, name="sums")
+            rotated_end = rotated_pool.tile([P, 2, HEAD], F32)
+            add_last_tile(b, turned, rotated_end[:])
+            end_tiles[b] = rotated_end
+
+        def store_end(b, w):
+            rows = (out_0, out_1)[w][b].rearrange("(p r) f -> p r f", r=ROWS)
+            nc.sync.dma_start(out=rows[:, LAST, :], in_=end_tiles[b][:, w, :])
+            nc.sync.dma_start(out=rows[:, 0:LAST, :], in_=rotated_tiles[b][:, w, 0:LAST, :])
+
         def finish(b):
             add(b, slice(0, 2), nc.gpsimd)
 
         def finish_store(b):
-            add_last_tile(b)
+            turned = turned_pool.tile([P, 2, HEAD], F32)
+            add_last_tile(b, turned, rotated_tiles[b][:, :, LAST, :])
             for w, out in enumerate((out_0, out_1)):
                 store(b, w, out)
             if b + X_CHUNKS_IN_SBUF < BATCH:
@@ -283,8 +296,16 @@ def tile_head_pa_kernel(tc, x, Wq, Wk, out_0, out_1):
         identity = const.tile([P, P], F32)
         swap = const.tile([P, P], F32)
 
+        warm = const.tile([P, 1], F32)
+        nc.gpsimd.memset(warm[:], 0.0)
+        nc.scalar.activation(out=warm[:], in_=warm[:], func=ACT.Sin)
+        load(0, slice(0, 1))
         w_rows = load_weights(nc, const, (Wq, Wk))
-        for b in range(X_CHUNKS_IN_SBUF):
+        for r in range(1, ROWS):
+            load(0, slice(r, r + 1))
+        for r in range(ROWS):
+            load(1, slice(r, r + 1))
+        for b in range(2, X_CHUNKS_IN_SBUF):
             load(b)
         signed = signed_turns(nc, const)
         make_identity(nc, identity[:])
@@ -293,12 +314,17 @@ def tile_head_pa_kernel(tc, x, Wq, Wk, out_0, out_1):
         )
         signed_by_feature = turned_pool.tile([P, 2, HEAD], F32, name="turned")
         nc.tensor.transpose(signed_by_feature[:, 0, :], signed[:].rearrange("p i h -> p (i h)"), identity[:])
-        half = half_angle_sines(nc, const, signed, signed_by_feature[:, 0, :])
-        quantise_weights(nc, const, w_rows, w_codes, w_scales)
+        minus = minus_turns(nc, const, signed, signed_by_feature[:, 0, :])
+        w_grouped = group_weights(nc, const, w_rows)
+        transpose(0, (0,))
+        half = half_angle_sines(nc, const, minus)
+        nc.vector.quantize_mx(
+            out=w_codes[:].bitcast(FP8X4), scales=w_scales[:], in_=w_grouped[:].rearrange("p g w f t -> p (g w f t)")
+        )
 
         first, second = range(0, 1), range(1, 2)
         both = range(0, 2)
-        transpose(0, (0, 1))
+        transpose(0, (1,))
         nc.scalar.activation(out=half[:], in_=half[:], func=ACT.Square)
         transpose(0, (2, 3))
         quantise(0, first)
@@ -321,25 +347,36 @@ def tile_head_pa_kernel(tc, x, Wq, Wk, out_0, out_1):
         finish(1)
         transpose(3)
         finish_store(0)
+        transpose(4)
         project(2, both)
         quantise(3, both)
-        for b in range(2, BATCH):
+        for b in range(2, BATCH - 2):
             multiply(b, 0)
             multiply(b, 1)
-            if b + 2 < BATCH:
-                transpose(b + 2)
-                finish_store(b - 1)
-                project(b + 1, both)
-                quantise(b + 2, both)
-                finish(b)
-            elif b + 1 < BATCH:
-                finish_store(b - 1)
-                project(b + 1, both)
-                finish(b)
-            else:
-                finish_store(b - 1)
-                for w, out in enumerate((out_0, out_1)):
-                    add(b, slice(w, w + 1), nc.vector)
-                add_last_tile(b)
-                for w, out in enumerate((out_0, out_1)):
-                    store(b, w, out)
+            if b + 3 < BATCH:
+                transpose(b + 3, (0, 1))
+            project(b + 1, first)
+            if b + 3 < BATCH:
+                transpose(b + 3, (2, 3))
+            finish_store(b - 1)
+            project(b + 1, second)
+            quantise(b + 2, both)
+            finish(b)
+        b = BATCH - 2
+        multiply(b, 0)
+        multiply(b, 1)
+        finish_store(b - 1)
+        project(b + 1, (1, 0))
+        for w in range(2):
+            add(b, slice(w, w + 1), nc.gpsimd)
+        last_tile_end(b)
+        for w in range(2):
+            store_end(b, w)
+        b = BATCH - 1
+        multiply(b, 1)
+        last_tile_end(b)
+        for w in range(2):
+            multiply(b, 0, slice(w, w + 1))
+        for w in range(2):
+            add(b, slice(w, w + 1), nc.vector)
+            store_end(b, w)

@@ -354,12 +354,9 @@ def tile_head_pa_kernel(tc, x, Wq, Wk, out_0, out_1):
             multiply(b, 0)
             multiply(b, 1)
             if b + 3 < BATCH:
-                transpose(b + 3, (0, 1))
-            project(b + 1, first)
-            if b + 3 < BATCH:
-                transpose(b + 3, (2, 3))
+                transpose(b + 3)
             finish_store(b - 1)
-            project(b + 1, second)
+            project(b + 1, both)
             quantise(b + 2, both)
             finish(b)
         b = BATCH - 2

@@ -105,8 +105,8 @@ def fill_rotation_table(nc, squares, table):
     nc.vector.tensor_scalar(
         out=pairs[:, 0:LAST, 1, :, 0], in0=by_token[:, 1], scalar1=2.0, scalar2=-1.0, op0=ALU.mult, op1=ALU.add
     )
-    nc.scalar.activation(
-        out=table[:, LAST], in_=squares[:, :, LAST * PAIRS : ANGLES], func=ACT.Identity, scale=-2.0, bias=1.0
+    nc.vector.tensor_scalar(
+        out=table[:, LAST], in0=squares[:, :, LAST * PAIRS : ANGLES], scalar1=-2.0, scalar2=1.0, op0=ALU.mult, op1=ALU.add
     )
 
 
@@ -123,13 +123,11 @@ def load_weights(nc, pool, weights):
 def group_weights(nc, pool, w_rows):
     w_grouped = pool.tile([P, PASSES, 2, HEAD, PACK], BF16, align_bytes=64)
     for g in range(PASSES):
-        q_rows, k_rows = (
-            w_rows[:, w, PACK * g : PACK * (g + 1), :].rearrange("p t f -> p f t") for w in range(2)
-        )
-        nc.gpsimd.tensor_scalar(
-            out=w_grouped[:, g, 0], in0=q_rows, scalar1=1.0, scalar2=0.0, op0=ALU.mult, op1=ALU.add
-        )
-        nc.vector.tensor_copy(out=w_grouped[:, g, 1], in_=k_rows)
+        for w in range(2):
+            nc.vector.tensor_copy(
+                out=w_grouped[:, g, w],
+                in_=w_rows[:, w, PACK * g : PACK * (g + 1), :].rearrange("p t f -> p f t"),
+            )
     return w_grouped
 
 
@@ -296,12 +294,8 @@ def tile_head_pa_kernel(tc, x, Wq, Wk, out_0, out_1):
         identity = const.tile([P, P], F32)
         swap = const.tile([P, P], F32)
 
-        warm = const.tile([P, 1], F32)
-        nc.gpsimd.memset(warm[:], 0.0)
-        nc.scalar.activation(out=warm[:], in_=warm[:], func=ACT.Sin)
-        load(0, slice(0, 1))
         w_rows = load_weights(nc, const, (Wq, Wk))
-        for r in range(1, ROWS):
+        for r in range(ROWS):
             load(0, slice(r, r + 1))
         for r in range(ROWS):
             load(1, slice(r, r + 1))
@@ -316,7 +310,6 @@ def tile_head_pa_kernel(tc, x, Wq, Wk, out_0, out_1):
         nc.tensor.transpose(signed_by_feature[:, 0, :], signed[:].rearrange("p i h -> p (i h)"), identity[:])
         minus = minus_turns(nc, const, signed, signed_by_feature[:, 0, :])
         w_grouped = group_weights(nc, const, w_rows)
-        transpose(0, (0,))
         half = half_angle_sines(nc, const, minus)
         nc.vector.quantize_mx(
             out=w_codes[:].bitcast(FP8X4), scales=w_scales[:], in_=w_grouped[:].rearrange("p g w f t -> p (g w f t)")
@@ -324,7 +317,7 @@ def tile_head_pa_kernel(tc, x, Wq, Wk, out_0, out_1):
 
         first, second = range(0, 1), range(1, 2)
         both = range(0, 2)
-        transpose(0, (1,))
+        transpose(0, (0, 1))
         nc.scalar.activation(out=half[:], in_=half[:], func=ACT.Square)
         transpose(0, (2, 3))
         quantise(0, first)

from contextlib import ExitStack
import math

import concourse.mybir as mybir
from concourse.masks import make_identity

F32 = mybir.dt.float32
BF16 = mybir.dt.bfloat16
U32 = mybir.dt.uint32
U8 = mybir.dt.uint8
FP8X4 = mybir.dt.float8_e4m3fn_x4
ALU = mybir.AluOpType
ACT = mybir.ActivationFunctionType

BATCH, TOKENS, CHANNELS, HEAD = 16, 512, 1024, 128
P = 128
PACK = 4
PASSES = CHANNELS // (P * PACK)
ROWS = TOKENS // P
PAIRS = HEAD // 2
FEATURES = 2 * HEAD
WORDS = CHANNELS // 2
TILE_COLS = PASSES * P
TILES_PER_BANK = 2
BANKS = ROWS // TILES_PER_BANK
BANK_COLS = TILES_PER_BANK * TILE_COLS
LAST = ROWS - 1
ANGLES = LAST * PAIRS + P
X_CHUNKS_IN_SBUF = 8

FLOPS = 2 * BATCH * TOKENS * CHANNELS * FEATURES

RATIO = 10000.0 ** (-2.0 / PAIRS)
ROUND_TO_WHOLE = 1.5 * 2**23


def signed_turns(nc, pool):
    minus_ones = pool.tile([P, PAIRS, 2], F32)
    nc.vector.memset(minus_ones[:], -1.0)
    factors = pool.tile([P, PAIRS, 2], F32)
    nc.vector.memset(factors[:], 1.0)
    nc.vector.tensor_scalar_mul(out=factors[:, :, 0], in0=minus_ones[:, :, 0], scalar1=-RATIO)
    signed = pool.tile([P, PAIRS, 2], F32)
    nc.vector.tensor_tensor_scan(
        out=signed[:].rearrange("p i h -> p (i h)"),
        data0=factors[:].rearrange("p i h -> p (i h)"),
        data1=minus_ones[:].rearrange("p i h -> p (i h)"),
        initial=RATIO**-2 / (2.0 * math.pi),
        op0=ALU.mult,
        op1=ALU.mult,
    )
    return signed


def minus_turns(nc, pool, signed, signed_by_feature):
    position = pool.tile([P, LAST], F32)
    nc.gpsimd.iota(
        position[:], pattern=[[1, LAST]], base=0, channel_multiplier=ROWS, allow_small_or_imprecise_dtypes=True
    )
    position_last = pool.tile([P, P], F32)
    nc.gpsimd.iota(
        position_last[:], pattern=[[ROWS, P]], base=LAST, channel_multiplier=0, allow_small_or_imprecise_dtypes=True
    )
    shape = [P, LAST, PAIRS]
    turns = pool.tile([P, ANGLES], F32)
    nc.vector.tensor_tensor(
        out=turns[:, 0 : LAST * PAIRS].rearrange("p (r i) -> p r i", r=LAST),
        in0=signed[:, :, 1].unsqueeze(1).to_broadcast(shape),
        in1=position[:].unsqueeze(2).to_broadcast(shape),
        op=ALU.mult,
    )
    nc.vector.tensor_tensor(
        out=turns[:, LAST * PAIRS : ANGLES], in0=signed_by_feature, in1=position_last[:], op=ALU.mult
    )
    whole = pool.tile([P, ANGLES], F32)
    nc.vector.tensor_scalar_add(out=whole[:], in0=turns[:], scalar1=ROUND_TO_WHOLE)
    minus = pool.tile([P, ANGLES], F32)
    nc.vector.scalar_tensor_tensor(
        out=minus[:], in0=whole[:], scalar=ROUND_TO_WHOLE, in1=turns[:], op0=ALU.subtract, op1=ALU.subtract
    )
    return minus


def half_angle_sines(nc, pool, minus):
    half = pool.tile([P, 2, ANGLES], F32)
    nc.scalar.activation(out=half[:, 0], in_=minus[:], func=ACT.Sin, scale=math.pi)
    nc.scalar.activation(out=half[:, 1], in_=minus[:], func=ACT.Sin, scale=math.pi, bias=math.pi / 4.0)
    return half


def fill_rotation_table(nc, squares, table):
    by_token = squares[:, :, 0 : LAST * PAIRS].rearrange("p s (r i) -> p s r i", r=LAST)
    pairs = table[:].rearrange("p r a (i h) -> p r a i h", h=2)
    nc.vector.tensor_scalar(
        out=pairs[:, 0:LAST, 0],
        in0=by_token[:, 0].unsqueeze(3).to_broadcast([P, LAST, PAIRS, 2]),
        scalar1=-2.0,
        scalar2=1.0,
        op0=ALU.mult,
        op1=ALU.add,
    )
    nc.vector.tensor_scalar(
        out=pairs[:, 0:LAST, 1, :, 1], in0=by_token[:, 1], scalar1=-2.0, scalar2=1.0, op0=ALU.mult, op1=ALU.add
    )
    nc.vector.tensor_scalar(
        out=pairs[:, 0:LAST, 1, :, 0], in0=by_token[:, 1], scalar1=2.0, scalar2=-1.0, op0=ALU.mult, op1=ALU.add
    )
    nc.vector.tensor_scalar(
        out=table[:, LAST], in0=squares[:, :, LAST * PAIRS : ANGLES], scalar1=-2.0, scalar2=1.0, op0=ALU.mult, op1=ALU.add
    )


def load_weights(nc, pool, weights):
    w_rows = pool.tile([P, 2, PASSES * PACK, HEAD], BF16)
    for w, weight in enumerate(weights):
        nc.sync.dma_start(
            out=w_rows[:, w].rearrange("p (c e) f -> p c (e f)", e=2),
            in_=weight.rearrange("(c p e) f -> p c (e f)", p=P, e=2),
        )
    return w_rows


def group_weights(nc, pool, w_rows):
    w_grouped = pool.tile([P, PASSES, 2, HEAD, PACK], BF16, align_bytes=64)
    for g in range(PASSES):
        for w in range(2):
            nc.vector.tensor_copy(
                out=w_grouped[:, g, w],
                in_=w_rows[:, w, PACK * g : PACK * (g + 1), :].rearrange("p t f -> p f t"),
            )
    return w_grouped


def tile_head_pa_kernel(tc, x, Wq, Wk, out_0, out_1):
    nc = tc.nc
    with ExitStack() as ctx:
        ctx.enter_context(tc.manual_schedule())
        const = ctx.enter_context(tc.tile_pool(name="const", bufs=1))
        x_pool = ctx.enter_context(tc.tile_pool(name="x", bufs=X_CHUNKS_IN_SBUF))
        grouped_pool = ctx.enter_context(tc.tile_pool(name="grouped", bufs=5))
        codes_pool = ctx.enter_context(tc.tile_pool(name="codes", bufs=5))
        products_pool = ctx.enter_context(tc.tile_pool(name="products", bufs=3))
        rotated_pool = ctx.enter_context(tc.tile_pool(name="rotated", bufs=4))
        transposed_pool = ctx.enter_context(tc.psum_pool(name="transposed", bufs=ROWS))
        sums_pool = ctx.enter_context(tc.psum_pool(name="sums", bufs=3))
        turned_pool = ctx.enter_context(tc.psum_pool(name="turned", bufs=1))

        x_tiles = {}
        grouped_tiles = {}
        codes_tiles = {}
        sums_tiles = {}
        products_tiles = {}
        rotated_tiles = {}
        end_tiles = {}

        def load(b, tiles=slice(0, ROWS)):
            if b not in x_tiles:
                x_rows = x_pool.tile([P, ROWS * CHANNELS], BF16)
                x_tiles[b] = x_rows
            columns = slice(CHANNELS * tiles.start, CHANNELS * tiles.stop)
            nc.sync.dma_start(
                out=x_tiles[b][:, columns], in_=x[b].rearrange("(p r) k -> p (r k)", r=ROWS)[:, columns]
            )

        def transpose(b, tiles=range(ROWS)):
            x_words = x_tiles[b][:].bitcast(F32)
            if b not in grouped_tiles:
                grouped = grouped_pool.tile([P, ROWS * TILE_COLS * PACK], BF16, align_bytes=64)
                grouped_tiles[b] = grouped
            grouped_words = grouped_tiles[b][:].bitcast(F32)
            for r in tiles:
                transposed = transposed_pool.tile([P, WORDS // P, P], F32)
                for j in range(WORDS // P):
                    first = WORDS * r + P * j
                    nc.tensor.transpose(transposed[:, j, :], x_words[:, first : first + P], identity[:])
                nc.scalar.copy(
                    out=grouped_words[:, 2 * TILE_COLS * r : 2 * TILE_COLS * (r + 1)].rearrange(
                        "p (g c u) -> p g c u", g=PASSES, u=2
                    ),
                    in_=transposed[:].rearrange("p (g u) c -> p g c u", u=2),
                )

        def quantise(b, banks):
            if b not in codes_tiles:
                codes = codes_pool.tile([P, ROWS * TILE_COLS], U32, align_bytes=64)
                scales = codes_pool.tile([P, ROWS * TILE_COLS], U8, align_bytes=64)
                codes_tiles[b] = (codes, scales)
            codes, scales = codes_tiles[b]
            columns = slice(BANK_COLS * banks.start, BANK_COLS * banks.stop)
            nc.vector.quantize_mx(
                out=codes[:, columns].bitcast(FP8X4),
                scales=scales[:, columns],
                in_=grouped_tiles[b][:, PACK * columns.start : PACK * columns.stop],
            )

        def project(b, banks):
            codes, scales = codes_tiles[b]
            for o in banks:
                sums = sums_pool.tile([P, TILES_PER_BANK, FEATURES], F32)
                for n in range(TILES_PER_BANK):
                    r = TILES_PER_BANK * o + n
                    for w in (0, 1) if r == LAST else (0,):
                        for g in range(PASSES):
                            tokens = slice(TILE_COLS * r + P * g, TILE_COLS * r + P * (g + 1))
                            if r == LAST:
                                features = slice(FEATURES * g + HEAD * w, FEATURES * g + HEAD * (w + 1))
                                columns = slice(HEAD * w, HEAD * (w + 1))
                                left, right = (w_codes, w_scales, features), (codes, scales, tokens)
                            else:
                                features = slice(FEATURES * g, FEATURES * (g + 1))
                                columns = slice(0, FEATURES)
                                left, right = (codes, scales, tokens), (w_codes, w_scales, features)
                            nc.tensor.matmul_mx(
                                out=sums[:, n, columns],
                                lhsT=left[0][:, left[2]].bitcast(FP8X4),
                                lhsT_scale=left[1][:, left[2]],
                                rhs=right[0][:, right[2]].bitcast(FP8X4),
                                rhs_scale=right[1][:, right[2]],
                                start=(g == 0),
                                stop=(g == PASSES - 1),
                            )
                sums_tiles[b, o] = sums

        def multiply(b, o, weights=slice(0, 2)):
            if b not in products_tiles:
                products = products_pool.tile([P, ROWS, 2, 2, HEAD], F32)
                products_tiles[b] = products
            rows = slice(TILES_PER_BANK * o, TILES_PER_BANK * (o + 1))
            shape = [P, TILES_PER_BANK, weights.stop - weights.start, 2, HEAD]
            sums = sums_tiles[b, o][:].rearrange("p n (w f) -> p n w f", w=2)[:, :, weights]
            nc.vector.tensor_tensor(
                out=products_tiles[b][:, rows, weights],
                in0=sums.unsqueeze(3).to_broadcast(shape),
                in1=table[:, rows].unsqueeze(2).to_broadcast(shape),
                op=ALU.mult,
            )

        def add(b, weights, adder):
            if b not in rotated_tiles:
                rotated = rotated_pool.tile([P, 2, ROWS, HEAD], F32)
                rotated_tiles[b] = rotated
            products = products_tiles[b][:, 0:LAST, weights].rearrange("p r w a (i h) -> p r w a i h", h=2)
            adder.tensor_tensor(
                out=rotated_tiles[b][:, weights, 0:LAST].rearrange("p w r (i h) -> p r w i h", h=2),
                in0=products[:, :, :, 0],
                in1=products[:, :, :, 1, :, ::-1],
                op=ALU.add,
            )

        def add_last_tile(b, turned, rotated_last):
            for w in range(2):
                for a, order in enumerate((identity, swap)):
                    nc.tensor.matmul(
                        turned[:, w, 0:HEAD],
                        lhsT=products_tiles[b][:, LAST, w, a, :],
                        rhs=order[:],
                        start=(a == 0),
                        stop=(a == 1),
                        is_transpose=True,
                    )
            nc.scalar.copy(out=rotated_last, in_=turned[:, :, 0:HEAD])

        def store(b, w, out):
            nc.sync.dma_start(
                out=out[b].rearrange("(p r) f -> p (r f)", r=ROWS),
                in_=rotated_tiles[b][:, w].rearrange("p r f -> p (r f)"),
            )

        def last_tile_end(b):
            turned = sums_pool.tile([P, TILES_PER_BANK, FEATURES], F32, name="sums")
            rotated_end = rotated_pool.tile([P, 2, HEAD], F32)
            add_last_tile(b, turned, rotated_end[:])
            end_tiles[b] = rotated_end

        def store_end(b, w):
            rows = (out_0, out_1)[w][b].rearrange("(p r) f -> p r f", r=ROWS)
            nc.sync.dma_start(out=rows[:, LAST, :], in_=end_tiles[b][:, w, :])
            nc.sync.dma_start(out=rows[:, 0:LAST, :], in_=rotated_tiles[b][:, w, 0:LAST, :])

        def finish(b):
            add(b, slice(0, 2), nc.gpsimd)

        def finish_store(b):
            turned = turned_pool.tile([P, 2, HEAD], F32)
            add_last_tile(b, turned, rotated_tiles[b][:, :, LAST, :])
            for w, out in enumerate((out_0, out_1)):
                store(b, w, out)
            if b + X_CHUNKS_IN_SBUF < BATCH:
                load(b + X_CHUNKS_IN_SBUF)

        w_codes = const.tile([P, PASSES * FEATURES], U32, align_bytes=64)
        w_scales = const.tile([P, PASSES * FEATURES], U8, align_bytes=64)
        table = const.tile([P, ROWS, 2, HEAD], F32)
        identity = const.tile([P, P], F32)
        swap = const.tile([P, P], F32)

        w_rows = load_weights(nc, const, (Wq, Wk))
        for r in range(ROWS):
            load(0, slice(r, r + 1))
        for r in range(ROWS):
            load(1, slice(r, r + 1))
        for b in range(2, X_CHUNKS_IN_SBUF):
            load(b)
        signed = signed_turns(nc, const)
        make_identity(nc, identity[:])
        nc.gpsimd.tensor_copy(
            out=swap[:].rearrange("p (i h) -> p i h", h=2), in_=identity[:].rearrange("p (i h) -> p i h", h=2)[:, :, ::-1]
        )
        signed_by_feature = turned_pool.tile([P, 2, HEAD], F32, name="turned")
        nc.tensor.transpose(signed_by_feature[:, 0, :], signed[:].rearrange("p i h -> p (i h)"), identity[:])
        minus = minus_turns(nc, const, signed, signed_by_feature[:, 0, :])
        w_grouped = group_weights(nc, const, w_rows)
        half = half_angle_sines(nc, const, minus)
        nc.vector.quantize_mx(
            out=w_codes[:].bitcast(FP8X4), scales=w_scales[:], in_=w_grouped[:].rearrange("p g w f t -> p (g w f t)")
        )

        first, second = range(0, 1), range(1, 2)
        both = range(0, 2)
        transpose(0, (0, 1))
        nc.scalar.activation(out=half[:], in_=half[:], func=ACT.Square)
        transpose(0, (2, 3))
        quantise(0, first)
        fill_rotation_table(nc, half, table)
        quantise(0, second)
        transpose(1, (0, 1))
        project(0, first)
        transpose(1, (2, 3))
        project(0, second)
        multiply(0, 0)
        quantise(1, first)
        multiply(0, 1)
        finish(0)
        quantise(1, second)
        transpose(2)
        project(1, both)
        multiply(1, 0)
        multiply(1, 1)
        quantise(2, both)
        finish(1)
        transpose(3)
        finish_store(0)
        transpose(4)
        project(2, both)
        quantise(3, both)
        for b in range(2, BATCH - 2):
            multiply(b, 0)
            multiply(b, 1)
            if b + 3 < BATCH:
                transpose(b + 3)
            finish_store(b - 1)
            project(b + 1, both)
            quantise(b + 2, both)
            finish(b)
        b = BATCH - 2
        multiply(b, 0)
        multiply(b, 1)
        finish_store(b - 1)
        project(b + 1, (1, 0))
        for w in range(2):
            add(b, slice(w, w + 1), nc.gpsimd)
        last_tile_end(b)
        for w in range(2):
            store_end(b, w)
        b = BATCH - 1
        multiply(b, 1)
        last_tile_end(b)
        for w in range(2):
            multiply(b, 0, slice(w, w + 1))
        for w in range(2):
            add(b, slice(w, w + 1), nc.vector)
            store_end(b, w)
